import numpy as np
import ml_dtypes


def mxq(x, axis, fmt="e4m3"):
    dtype, down = {"e4m3": (ml_dtypes.float8_e4m3fn, 7), "e5m2": (ml_dtypes.float8_e5m2, 14)}[fmt]
    v = np.moveaxis(np.asarray(x, np.float32).astype(ml_dtypes.bfloat16).astype(np.float64), axis, -1)
    blocks = v.reshape(v.shape[:-1] + (-1, 32))
    amax = np.abs(blocks).max(-1, keepdims=True)
    byte = np.maximum(np.where(amax > 0, np.frexp(amax)[1] - 1 + 127, 0) - down, 1)
    scale = np.exp2(byte - 127.0)
    codes = (blocks / scale).astype(np.float32).astype(dtype).astype(np.float64)
    return np.moveaxis((codes * scale).reshape(v.shape), -1, axis)


WIDE = False


def mx_kscale(k):
    if not WIDE:
        return np.ones(k)
    levels = np.array([10, -10, 5, -5, 0])
    a = np.random.permutation(np.resize(levels, k // 512 * 4)).reshape(k // 512, 4)
    idx = np.arange(k)
    return np.exp2(a[idx // 512, idx % 128 // 32])


BF16 = ml_dtypes.bfloat16


def bf(x):
    return np.asarray(x, np.float32).astype(BF16)


def f64(x):
    return np.asarray(x).astype(np.float64)


E2M1 = np.array([0.0, 0.5, 1.0, 1.5, 2.0, 3.0, 4.0, 6.0, -0.0, -0.5, -1.0, -1.5, -2.0, -3.0, -4.0, -6.0])


def pack_weight(w, fmt):
    k, n = w.shape
    w = f64(bf(w)).reshape(k // 32, 32, n)
    amax = np.abs(w).max(1)
    if fmt == "e4m3":
        byte = np.frexp(amax)[1] - 1 + 127 - 7
    else:
        mant, ex = np.frexp(amax / 6.0)
        byte = np.where(mant > 0.5, ex, ex - 1) + 127
    byte = np.clip(np.where(amax > 0, byte, 1), 1, 254)
    scaled = (w * np.exp2(127.0 - byte)[:, None, :]).reshape(k, n).astype(np.float32)
    by_word = np.ascontiguousarray(scaled.reshape(k // 512, 128, 4, n).transpose(0, 1, 3, 2))
    if fmt == "e4m3":
        words = by_word.astype(ml_dtypes.float8_e4m3fn).view(np.uint8)
    else:
        c = by_word.astype(ml_dtypes.float4_e2m1fn).view(np.uint8) & 0xF
        words = c[..., 0::2] | (c[..., 1::2] << 4)
    return np.ascontiguousarray(words), np.ascontiguousarray(byte.astype(np.uint8).reshape(k // 512, 16, n))


def unpack_weight(words, scales, fmt):
    g, p, n, _ = words.shape
    if fmt == "e4m3":
        vals = np.ascontiguousarray(words).view(ml_dtypes.float8_e4m3fn).astype(np.float64)
    else:
        nib = np.empty((g, p, n, 4), np.uint8)
        nib[..., 0::2] = words & 0xF
        nib[..., 1::2] = words >> 4
        vals = E2M1[nib]
    vals = vals * np.repeat(np.exp2(scales.astype(np.float64) - 127.0), 8, axis=1)[..., None]
    return vals.transpose(0, 1, 3, 2).reshape(g * 512, n)

def pack4(w):
    words, scales = pack_weight(w, "e2m1")
    return words.reshape(words.shape[0], 128, -1), scales


def unpack4(words, scales):
    return unpack_weight(words.reshape(words.shape[0], 128, -1, 2), scales, "e2m1")


B, X_DIM, Z_DIM, K, H = 3072, 1024, 64, 512, 512


def elu(v):
    return np.where(v > 0.0, v, np.exp(np.minimum(v, 0.0)) - 1.0)


def softplus(v):
    return np.maximum(v, 0.0) + np.log(1.0 + np.exp(-np.abs(v)))


def setup_inputs():
    s = mx_kscale(H)
    dec_h1 = bf(elu(np.random.standard_normal((B, H))) * s)
    x = bf(np.random.random((B, X_DIM)))
    dw2_words, dw2_scales = pack4(np.random.standard_normal((H, H)) * 1.25 / np.sqrt(H) / s[:, None])
    db2 = bf(np.random.standard_normal(H) * 0.5)
    dw3_words, dw3_scales = pack4(np.random.standard_normal((H, X_DIM)) * 2.5 / np.sqrt(H))
    db3 = bf(np.random.standard_normal(X_DIM) * 0.8)
    return {"dec_h1": dec_h1,
            "x": x,
            "dw2_words": dw2_words,
            "dw2_scales": dw2_scales,
            "db2": db2,
            "dw3_words": dw3_words,
            "dw3_scales": dw3_scales,
            "db3": db3}


def reference(dec_h1, x, dw2_words, dw2_scales, db2, dw3_words, dw3_scales, db3):
    d2 = elu((mxq(f64(dec_h1), 1, "e4m3") @ unpack4(dw2_words, dw2_scales)) + f64(db2))
    logits = (mxq(d2, 1, "e4m3") @ unpack4(dw3_words, dw3_scales)) + f64(db3)
    return np.sum(f64(x) * logits - softplus(logits), axis=-1)

@@ -1,0 +1,315 @@
+from contextlib import ExitStack
+
+import concourse.mybir as mybir
+from concourse.masks import make_identity
+
+F32 = mybir.dt.float32
+BF16 = mybir.dt.bfloat16
+I32 = mybir.dt.int32
+U32 = mybir.dt.uint32
+U8 = mybir.dt.uint8
+FP8X4 = mybir.dt.float8_e4m3fn_x4
+FP4X4 = mybir.dt.float4_e2m1fn_x4
+ALU = mybir.AluOpType
+ACT = mybir.ActivationFunctionType
+
+P = 128
+PACK = 4
+BATCH, HIDDEN, PIXELS = 3072, 512, 1024
+N_TILES = BATCH // P
+BANK = 512
+HALVES = PIXELS // BANK
+LOAD_TILES = 4
+GROUP = 12
+ABS_ON_SCALAR = 512
+
+FLOPS = 2 * BATCH * HIDDEN * (HIDDEN + PIXELS)
+
+LAG_COPY_H, LAG_QUANT_H, LAG_BIAS, LAG_EXP, LAG_ELU, LAG_COPY_D, LAG_QUANT_D = 1, 2, 3, 4, 5, 6, 7
+
+
+def tile_gmvae_pb_kernel(
+    tc, dec_h1, x, dw2_words, dw2_scales, db2, dw3_words, dw3_scales, db3, out
+):
+    nc = tc.nc
+    h_rows = dec_h1.rearrange("(p i) k -> p i k", i=N_TILES)
+    x_rows = x.rearrange("(p i) j -> p i j", i=N_TILES)
+
+    with ExitStack() as stack:
+        stack.enter_context(tc.manual_schedule())
+        keep = stack.enter_context(tc.tile_pool(name="keep", bufs=1))
+        banks = stack.enter_context(tc.psum_pool(name="banks", bufs=8))
+
+        planes = keep.tile([P, HIDDEN + PIXELS], U8, align_bytes=64)
+        planes_i32 = planes[:].bitcast(I32)
+        nc.vector.memset(planes_i32, 0)
+        ident = keep.tile([P, P], F32)
+        make_identity(nc, ident[:])
+
+        h_loads = []
+        x_loads = []
+        for c in range(N_TILES // LOAD_TILES):
+            h_loads.append(keep.tile([P, LOAD_TILES, HIDDEN], BF16, name="h_load%d" % c))
+            x_loads.append(keep.tile([P, LOAD_TILES, PIXELS], BF16, name="x_load%d" % c))
+        w2 = keep.tile([P, 2 * HIDDEN], U8, align_bytes=64)
+        w3 = keep.tile([P, 2 * PIXELS], U8, align_bytes=64)
+        b2_rows = keep.tile([P, HIDDEN], BF16)
+        b3_rows = keep.tile([P, PIXELS], BF16)
+
+        def load_scales(scales, first_col):
+            rows = scales.rearrange("g q n -> (g q) n").bitcast(I32)
+            width = rows.shape[1]
+            for r in range(4):
+                nc.sync.dma_start(
+                    out=planes_i32[r:P:32, first_col // 4 : first_col // 4 + width],
+                    in_=rows[r:16:4, :],
+                )
+
+        nc.scalar.dma_start(out=b2_rows[:], in_=db2.partition_broadcast(P))
+        nc.sync.dma_start(out=h_loads[0][:], in_=h_rows[:, 0:LOAD_TILES, :])
+        nc.sync.dma_start(
+            out=w2[:].bitcast(I32), in_=dw2_words.rearrange("g p n -> (g p) n").bitcast(I32)
+        )
+        load_scales(dw2_scales, 0)
+        for c in range(1, N_TILES // LOAD_TILES):
+            nc.sync.dma_start(
+                out=h_loads[c][:], in_=h_rows[:, c * LOAD_TILES : (c + 1) * LOAD_TILES, :]
+            )
+        nc.sync.dma_start(
+            out=w3[:].bitcast(I32), in_=dw3_words.rearrange("g p n -> (g p) n").bitcast(I32)
+        )
+        load_scales(dw3_scales, HIDDEN)
+        nc.sync.dma_start(out=b3_rows[:], in_=db3.partition_broadcast(P))
+        for c in range(N_TILES // LOAD_TILES):
+            nc.sync.dma_start(
+                out=x_loads[c][:], in_=x_rows[:, c * LOAD_TILES : (c + 1) * LOAD_TILES, :]
+            )
+
+        b2_plus1 = keep.tile([P, PACK, P], F32)
+        nc.vector.tensor_scalar(
+            out=b2_plus1[:],
+            in0=b2_rows[:].rearrange("p (q t) -> p t q", t=PACK),
+            scalar1=1.0,
+            scalar2=None,
+            op0=ALU.add,
+        )
+
+        d_codes = keep.tile([P, BATCH], U32, align_bytes=64)
+        d_scales = keep.tile([P, BATCH], U8, align_bytes=64)
+
+        with ExitStack() as stage1:
+            hold = stage1.enter_context(tc.tile_pool(name="hold", bufs=1))
+            ring3 = stage1.enter_context(tc.tile_pool(name="ring3", bufs=3))
+            ring4 = stage1.enter_context(tc.tile_pool(name="ring4", bufs=4))
+            h_codes = hold.tile([P, BATCH], U32, align_bytes=64)
+            h_scales = hold.tile([P, BATCH], U8, align_bytes=64)
+            live = {}
+
+            def transpose_h(i):
+                words = h_loads[i // LOAD_TILES][:, i % LOAD_TILES, :].bitcast(F32)
+                h_t = banks.tile([P, 2, P], F32, tag="bank", name="h_t")
+                for u in range(2):
+                    nc.tensor.transpose(h_t[:, u, :], words[:, u : HIDDEN // 2 : 2], ident[:])
+                live["h_t", i] = h_t
+
+            def copy_h(i):
+                h_grouped = ring3.tile([P, PACK * P], BF16, align_bytes=64, name="h_grouped")
+                nc.scalar.copy(
+                    out=h_grouped[:].bitcast(F32).rearrange("p (r u) -> p r u", u=2),
+                    in_=live.pop(("h_t", i))[:].rearrange("p u r -> p r u"),
+                )
+                live["h_grouped", i] = h_grouped
+
+            def quantise_h(i):
+                cols = slice(i * P, (i + 1) * P)
+                nc.vector.quantize_mx(
+                    out=h_codes[:, cols].bitcast(FP8X4),
+                    scales=h_scales[:, cols],
+                    in_=live.pop(("h_grouped", i))[:],
+                )
+
+            def hidden_matmul(i):
+                cols = slice(i * P, (i + 1) * P)
+                acc = banks.tile([P, BANK], F32, tag="bank", name="acc1")
+                nc.tensor.matmul_mx(
+                    out=acc[:],
+                    lhsT=h_codes[:, cols].bitcast(FP8X4),
+                    lhsT_scale=h_scales[:, cols],
+                    rhs=w2[:].bitcast(FP4X4),
+                    rhs_scale=planes[:, 0:HIDDEN],
+                    start=True,
+                    stop=True,
+                )
+                live["acc1", i] = acc
+
+            def add_bias(i):
+                v_plus1 = ring4.tile([P, PACK, P], F32, name="v_plus1")
+                nc.vector.tensor_tensor(
+                    out=v_plus1[:],
+                    in0=live.pop(("acc1", i))[:].rearrange("p (q t) -> p t q", t=PACK),
+                    in1=b2_plus1[:],
+                    op=ALU.add,
+                )
+                live["v_plus1", i] = v_plus1
+
+            def exp_v(i):
+                exp_of_v = ring3.tile([P, PACK, P], F32, name="exp_of_v")
+                nc.scalar.activation(
+                    out=exp_of_v[:], in_=live["v_plus1", i][:], func=ACT.Exp, bias=-1.0
+                )
+                live["exp_of_v", i] = exp_of_v
+
+            def elu_plus1(i):
+                d_plus1 = ring3.tile([P, PACK, P], F32, name="d_plus1")
+                nc.vector.scalar_tensor_tensor(
+                    out=d_plus1[:],
+                    in0=live.pop(("exp_of_v", i))[:],
+                    scalar=1.0,
+                    in1=live.pop(("v_plus1", i))[:],
+                    op0=ALU.min,
+                    op1=ALU.max,
+                )
+                live["d_plus1", i] = d_plus1
+
+            def transpose_d(i):
+                d_plus1 = live.pop(("d_plus1", i))
+                d_t = banks.tile([P, PACK, P], F32, tag="bank", name="d_t")
+                for t in range(PACK):
+                    nc.tensor.transpose(d_t[:, t, :], d_plus1[:, t, :], ident[:])
+                live["d_t", i] = d_t
+
+            def copy_d(i):
+                d_grouped = ring3.tile([P, P, PACK], BF16, align_bytes=64, name="d_grouped")
+                nc.scalar.activation(
+                    out=d_grouped[:],
+                    in_=live.pop(("d_t", i))[:].rearrange("p t r -> p r t"),
+                    func=ACT.Identity,
+                    bias=-1.0,
+                )
+                live["d_grouped", i] = d_grouped
+
+            def quantise_d(i):
+                cols = slice(i * P, (i + 1) * P)
+                nc.vector.quantize_mx(
+                    out=d_codes[:, cols].bitcast(FP8X4),
+                    scales=d_scales[:, cols],
+                    in_=live.pop(("d_grouped", i))[:].rearrange("p r t -> p (r t)"),
+                )
+
+            def in_range(i):
+                return 0 <= i < N_TILES
+
+            for n in range(N_TILES + LAG_QUANT_D):
+                if in_range(n - LAG_QUANT_H):
+                    quantise_h(n - LAG_QUANT_H)
+                    hidden_matmul(n - LAG_QUANT_H)
+                if in_range(n - LAG_BIAS):
+                    add_bias(n - LAG_BIAS)
+                if in_range(n - LAG_COPY_H):
+                    copy_h(n - LAG_COPY_H)
+                if in_range(n - LAG_ELU):
+                    elu_plus1(n - LAG_ELU)
+                    transpose_d(n - LAG_ELU)
+                if in_range(n - LAG_EXP):
+                    exp_v(n - LAG_EXP)
+                if in_range(n - LAG_QUANT_D):
+                    quantise_d(n - LAG_QUANT_D)
+                if in_range(n - LAG_COPY_D):
+                    copy_d(n - LAG_COPY_D)
+                if in_range(n):
+                    transpose_h(n)
+
+        sum_xl = keep.tile([P, N_TILES], F32)
+        sum_abs_vector = keep.tile([P, N_TILES], F32)
+        sum_abs_scalar = keep.tile([P, N_TILES], F32)
+        sum_log = keep.tile([P, N_TILES], F32)
+        group_pool = stack.enter_context(tc.tile_pool(name="group", bufs=GROUP))
+        logit_tiles = {}
+        abs_tiles = {}
+
+        def logits(i):
+            cols = slice(i * P, (i + 1) * P)
+            logit = group_pool.tile([P, PIXELS], F32, name="logit")
+            for c in range(HALVES):
+                acc = banks.tile([P, BANK], F32, tag="bank", name="acc2")
+                nc.tensor.matmul_mx(
+                    out=acc[:],
+                    lhsT=d_codes[:, cols].bitcast(FP8X4),
+                    lhsT_scale=d_scales[:, cols],
+                    rhs=w3[:, c * 2 * BANK : (c + 1) * 2 * BANK].bitcast(FP4X4),
+                    rhs_scale=planes[:, HIDDEN + c * BANK : HIDDEN + (c + 1) * BANK],
+                    start=True,
+                    stop=True,
+                )
+                nc.vector.tensor_tensor(
+                    out=logit[:, c * BANK : (c + 1) * BANK],
+                    in0=acc[:],
+                    in1=b3_rows[:, c * BANK : (c + 1) * BANK],
+                    op=ALU.add,
+                )
+            logit_tiles[i] = logit
+
+        def absolute(i):
+            logit = logit_tiles[i]
+            abs_l = group_pool.tile([P, PIXELS], F32, name="abs_l")
+            nc.vector.scalar_tensor_tensor(
+                out=abs_l[:, ABS_ON_SCALAR:],
+                in0=logit[:, ABS_ON_SCALAR:],
+                scalar=-1.0,
+                in1=logit[:, ABS_ON_SCALAR:],
+                op0=ALU.mult,
+                op1=ALU.max,
+                accum_out=sum_abs_vector[:, i : i + 1],
+            )
+            nc.scalar.activation(
+                out=abs_l[:, :ABS_ON_SCALAR],
+                in_=logit[:, :ABS_ON_SCALAR],
+                func=ACT.Abs,
+                accum_out=sum_abs_scalar[:, i : i + 1],
+            )
+            abs_tiles[i] = abs_l
+
+        def exp_minus_abs(i):
+            nc.scalar.activation(out=abs_tiles[i][:], in_=abs_tiles[i][:], func=ACT.Exp, scale=-1.0)
+
+        def dot_with_x(i):
+            logit = logit_tiles.pop(i)
+            nc.vector.scalar_tensor_tensor(
+                out=logit[:],
+                in0=x_loads[i // LOAD_TILES][:, i % LOAD_TILES, :],
+                scalar=-0.5,
+                in1=logit[:],
+                op0=ALU.add,
+                op1=ALU.mult,
+                accum_out=sum_xl[:, i : i + 1],
+            )
+
+        def log1p(i):
+            e = abs_tiles.pop(i)
+            nc.scalar.activation(
+                out=e[:], in_=e[:], func=ACT.Ln, bias=1.0, accum_out=sum_log[:, i : i + 1]
+            )
+
+        for first in range(0, N_TILES, GROUP):
+            for n in range(GROUP + 2):
+                if n < GROUP:
+                    logits(first + n)
+                if 1 <= n <= GROUP:
+                    absolute(first + n - 1)
+                if n >= 2:
+                    exp_minus_abs(first + n - 2)
+            for i in range(first, first + GROUP):
+                dot_with_x(i)
+                log1p(i)
+
+        sum_abs = keep.tile([P, N_TILES], F32)
+        nc.vector.tensor_tensor(
+            out=sum_abs[:], in0=sum_abs_vector[:], in1=sum_abs_scalar[:], op=ALU.add
+        )
+        linear = keep.tile([P, N_TILES], F32)
+        nc.vector.scalar_tensor_tensor(
+            out=linear[:], in0=sum_abs[:], scalar=-0.5, in1=sum_xl[:], op0=ALU.mult, op1=ALU.add
+        )
+        result = keep.tile([P, N_TILES], F32)
+        nc.vector.tensor_tensor(out=result[:], in0=linear[:], in1=sum_log[:], op=ALU.subtract)
+        nc.sync.dma_start(out=out.rearrange("(p i) -> p i", i=N_TILES), in_=result[:])

@@ -19,13 +19,23 @@ BATCH, HIDDEN, PIXELS = 3072, 512, 1024
 N_TILES = BATCH // P
 BANK = 512
 HALVES = PIXELS // BANK
+PAIR = 2
+N_PAIRS = N_TILES // PAIR
 LOAD_TILES = 4
 GROUP = 12
-ABS_ON_SCALAR = 512
+ABS_ON_SCALAR = 576
 
 FLOPS = 2 * BATCH * HIDDEN * (HIDDEN + PIXELS)
 
-LAG_COPY_H, LAG_QUANT_H, LAG_BIAS, LAG_EXP, LAG_ELU, LAG_COPY_D, LAG_QUANT_D = 1, 2, 3, 4, 5, 6, 7
+LAG_COPY_H = 1
+LAG_QUANT_H = 2
+LAG_HIDDEN = 2
+LAG_EXP = 3
+LAG_ELU = 4
+LAG_COPY_D = 5
+LAG_LOGITS = 6
+LAG_ABS = 7
+LAG_EXP_ABS = 8
 
 
 def tile_gmvae_pb_kernel(
@@ -38,7 +48,15 @@ def tile_gmvae_pb_kernel(
     with ExitStack() as stack:
         stack.enter_context(tc.manual_schedule())
         keep = stack.enter_context(tc.tile_pool(name="keep", bufs=1))
-        banks = stack.enter_context(tc.psum_pool(name="banks", bufs=8))
+        ring2 = stack.enter_context(tc.tile_pool(name="ring2", bufs=2))
+        ring3 = stack.enter_context(tc.tile_pool(name="ring3", bufs=3))
+        logit_pool = stack.enter_context(
+            tc.tile_pool(name="logit", bufs=GROUP + LAG_EXP_ABS - LAG_LOGITS)
+        )
+        abs_pool = stack.enter_context(
+            tc.tile_pool(name="abs", bufs=GROUP + LAG_EXP_ABS - LAG_ABS)
+        )
+        banks = stack.enter_context(tc.psum_pool(name="banks", bufs=2))
 
         planes = keep.tile([P, HIDDEN + PIXELS], U8, align_bytes=64)
         planes_i32 = planes[:].bitcast(I32)
@@ -47,9 +65,10 @@ def tile_gmvae_pb_kernel(
         make_identity(nc, ident[:])
 
         h_loads = []
+        for j in range(N_PAIRS):
+            h_loads.append(keep.tile([P, PAIR, HIDDEN], BF16, name="h_load%d" % j))
         x_loads = []
         for c in range(N_TILES // LOAD_TILES):
-            h_loads.append(keep.tile([P, LOAD_TILES, HIDDEN], BF16, name="h_load%d" % c))
             x_loads.append(keep.tile([P, LOAD_TILES, PIXELS], BF16, name="x_load%d" % c))
         w2 = keep.tile([P, 2 * HIDDEN], U8, align_bytes=64)
         w3 = keep.tile([P, 2 * PIXELS], U8, align_bytes=64)
@@ -65,25 +84,32 @@ def tile_gmvae_pb_kernel(
                     in_=rows[r:16:4, :],
                 )
 
+        def load_h(j):
+            nc.sync.dma_start(out=h_loads[j][:], in_=h_rows[:, j * PAIR : (j + 1) * PAIR, :])
+
         nc.scalar.dma_start(out=b2_rows[:], in_=db2.partition_broadcast(P))
-        nc.sync.dma_start(out=h_loads[0][:], in_=h_rows[:, 0:LOAD_TILES, :])
+        load_h(0)
         nc.sync.dma_start(
             out=w2[:].bitcast(I32), in_=dw2_words.rearrange("g p n -> (g p) n").bitcast(I32)
         )
         load_scales(dw2_scales, 0)
-        for c in range(1, N_TILES // LOAD_TILES):
-            nc.sync.dma_start(
-                out=h_loads[c][:], in_=h_rows[:, c * LOAD_TILES : (c + 1) * LOAD_TILES, :]
-            )
+        for j in range(1, 4):
+            load_h(j)
         nc.sync.dma_start(
             out=w3[:].bitcast(I32), in_=dw3_words.rearrange("g p n -> (g p) n").bitcast(I32)
         )
         load_scales(dw3_scales, HIDDEN)
         nc.sync.dma_start(out=b3_rows[:], in_=db3.partition_broadcast(P))
+        for j in range(4, N_PAIRS):
+            load_h(j)
         for c in range(N_TILES // LOAD_TILES):
             nc.sync.dma_start(
                 out=x_loads[c][:], in_=x_rows[:, c * LOAD_TILES : (c + 1) * LOAD_TILES, :]
             )
+
+        warm = keep.tile([P, 2], F32)
+        nc.vector.memset(warm[:], 0.0)
+        nc.scalar.activation(out=warm[:, 1:2], in_=warm[:, 0:1], func=ACT.Exp)
 
         b2_plus1 = keep.tile([P, PACK, P], F32)
         nc.vector.tensor_scalar(
@@ -94,164 +120,130 @@ def tile_gmvae_pb_kernel(
             op0=ALU.add,
         )
 
-        d_codes = keep.tile([P, BATCH], U32, align_bytes=64)
-        d_scales = keep.tile([P, BATCH], U8, align_bytes=64)
-
-        with ExitStack() as stage1:
-            hold = stage1.enter_context(tc.tile_pool(name="hold", bufs=1))
-            ring3 = stage1.enter_context(tc.tile_pool(name="ring3", bufs=3))
-            ring4 = stage1.enter_context(tc.tile_pool(name="ring4", bufs=4))
-            h_codes = hold.tile([P, BATCH], U32, align_bytes=64)
-            h_scales = hold.tile([P, BATCH], U8, align_bytes=64)
-            live = {}
-
-            def transpose_h(i):
-                words = h_loads[i // LOAD_TILES][:, i % LOAD_TILES, :].bitcast(F32)
-                h_t = banks.tile([P, 2, P], F32, tag="bank", name="h_t")
-                for u in range(2):
-                    nc.tensor.transpose(h_t[:, u, :], words[:, u : HIDDEN // 2 : 2], ident[:])
-                live["h_t", i] = h_t
-
-            def copy_h(i):
-                h_grouped = ring3.tile([P, PACK * P], BF16, align_bytes=64, name="h_grouped")
-                nc.scalar.copy(
-                    out=h_grouped[:].bitcast(F32).rearrange("p (r u) -> p r u", u=2),
-                    in_=live.pop(("h_t", i))[:].rearrange("p u r -> p r u"),
-                )
-                live["h_grouped", i] = h_grouped
-
-            def quantise_h(i):
-                cols = slice(i * P, (i + 1) * P)
-                nc.vector.quantize_mx(
-                    out=h_codes[:, cols].bitcast(FP8X4),
-                    scales=h_scales[:, cols],
-                    in_=live.pop(("h_grouped", i))[:],
-                )
-
-            def hidden_matmul(i):
-                cols = slice(i * P, (i + 1) * P)
-                acc = banks.tile([P, BANK], F32, tag="bank", name="acc1")
-                nc.tensor.matmul_mx(
-                    out=acc[:],
-                    lhsT=h_codes[:, cols].bitcast(FP8X4),
-                    lhsT_scale=h_scales[:, cols],
-                    rhs=w2[:].bitcast(FP4X4),
-                    rhs_scale=planes[:, 0:HIDDEN],
-                    start=True,
-                    stop=True,
-                )
-                live["acc1", i] = acc
-
-            def add_bias(i):
-                v_plus1 = ring4.tile([P, PACK, P], F32, name="v_plus1")
-                nc.vector.tensor_tensor(
-                    out=v_plus1[:],
-                    in0=live.pop(("acc1", i))[:].rearrange("p (q t) -> p t q", t=PACK),
-                    in1=b2_plus1[:],
-                    op=ALU.add,
-                )
-                live["v_plus1", i] = v_plus1
-
-            def exp_v(i):
-                exp_of_v = ring3.tile([P, PACK, P], F32, name="exp_of_v")
-                nc.scalar.activation(
-                    out=exp_of_v[:], in_=live["v_plus1", i][:], func=ACT.Exp, bias=-1.0
-                )
-                live["exp_of_v", i] = exp_of_v
-
-            def elu_plus1(i):
-                d_plus1 = ring3.tile([P, PACK, P], F32, name="d_plus1")
-                nc.vector.scalar_tensor_tensor(
-                    out=d_plus1[:],
-                    in0=live.pop(("exp_of_v", i))[:],
-                    scalar=1.0,
-                    in1=live.pop(("v_plus1", i))[:],
-                    op0=ALU.min,
-                    op1=ALU.max,
-                )
-                live["d_plus1", i] = d_plus1
-
-            def transpose_d(i):
-                d_plus1 = live.pop(("d_plus1", i))
-                d_t = banks.tile([P, PACK, P], F32, tag="bank", name="d_t")
-                for t in range(PACK):
-                    nc.tensor.transpose(d_t[:, t, :], d_plus1[:, t, :], ident[:])
-                live["d_t", i] = d_t
-
-            def copy_d(i):
-                d_grouped = ring3.tile([P, P, PACK], BF16, align_bytes=64, name="d_grouped")
-                nc.scalar.activation(
-                    out=d_grouped[:],
-                    in_=live.pop(("d_t", i))[:].rearrange("p t r -> p r t"),
-                    func=ACT.Identity,
-                    bias=-1.0,
-                )
-                live["d_grouped", i] = d_grouped
-
-            def quantise_d(i):
-                cols = slice(i * P, (i + 1) * P)
-                nc.vector.quantize_mx(
-                    out=d_codes[:, cols].bitcast(FP8X4),
-                    scales=d_scales[:, cols],
-                    in_=live.pop(("d_grouped", i))[:].rearrange("p r t -> p (r t)"),
-                )
-
-            def in_range(i):
-                return 0 <= i < N_TILES
-
-            for n in range(N_TILES + LAG_QUANT_D):
-                if in_range(n - LAG_QUANT_H):
-                    quantise_h(n - LAG_QUANT_H)
-                    hidden_matmul(n - LAG_QUANT_H)
-                if in_range(n - LAG_BIAS):
-                    add_bias(n - LAG_BIAS)
-                if in_range(n - LAG_COPY_H):
-                    copy_h(n - LAG_COPY_H)
-                if in_range(n - LAG_ELU):
-                    elu_plus1(n - LAG_ELU)
-                    transpose_d(n - LAG_ELU)
-                if in_range(n - LAG_EXP):
-                    exp_v(n - LAG_EXP)
-                if in_range(n - LAG_QUANT_D):
-                    quantise_d(n - LAG_QUANT_D)
-                if in_range(n - LAG_COPY_D):
-                    copy_d(n - LAG_COPY_D)
-                if in_range(n):
-                    transpose_h(n)
-
         sum_xl = keep.tile([P, N_TILES], F32)
         sum_abs_vector = keep.tile([P, N_TILES], F32)
         sum_abs_scalar = keep.tile([P, N_TILES], F32)
         sum_log = keep.tile([P, N_TILES], F32)
-        group_pool = stack.enter_context(tc.tile_pool(name="group", bufs=GROUP))
-        logit_tiles = {}
-        abs_tiles = {}
+        live = {}
 
-        def logits(i):
+        h_codes = keep.tile([P, BATCH], U32, align_bytes=64)
+        h_scales = keep.tile([P, BATCH], U8, align_bytes=64)
+
+        def transpose_h(j):
+            h_t = banks.tile([P, PAIR, 2, P], F32, name="h_t")
+            for s in range(PAIR):
+                words = h_loads[j][:, s, :].bitcast(F32)
+                for u in range(2):
+                    nc.tensor.transpose(h_t[:, s, u, :], words[:, u : HIDDEN // 2 : 2], ident[:])
+            live["h_t", j] = h_t
+
+        def copy_h(j):
+            h_grouped = ring2.tile([P, PAIR * P * PACK], BF16, align_bytes=64, name="h_grouped")
+            nc.scalar.copy(
+                out=h_grouped[:].bitcast(F32).rearrange("p (s r u) -> p s r u", s=PAIR, u=2),
+                in_=live.pop(("h_t", j))[:].rearrange("p s u r -> p s r u"),
+            )
+            live["h_grouped", j] = h_grouped
+
+        def quantise_h(j):
+            cols = slice(j * PAIR * P, (j + 1) * PAIR * P)
+            nc.vector.quantize_mx(
+                out=h_codes[:, cols].bitcast(FP8X4),
+                scales=h_scales[:, cols],
+                in_=live.pop(("h_grouped", j))[:],
+            )
+
+        def hidden_matmul(i):
             cols = slice(i * P, (i + 1) * P)
-            logit = group_pool.tile([P, PIXELS], F32, name="logit")
+            acc = banks.tile([P, BANK], F32, name="acc1")
+            nc.tensor.matmul_mx(
+                out=acc[:],
+                lhsT=h_codes[:, cols].bitcast(FP8X4),
+                lhsT_scale=h_scales[:, cols],
+                rhs=w2[:].bitcast(FP4X4),
+                rhs_scale=planes[:, 0:HIDDEN],
+                start=True,
+                stop=True,
+            )
+            live["acc1", i] = acc
+
+        def add_bias2(i):
+            v_plus1 = ring3.tile([P, PACK, P], F32, name="v_plus1")
+            nc.vector.tensor_tensor(
+                out=v_plus1[:],
+                in0=live.pop(("acc1", i))[:].rearrange("p (q t) -> p t q", t=PACK),
+                in1=b2_plus1[:],
+                op=ALU.add,
+            )
+            live["v_plus1", i] = v_plus1
+
+        def exp_v(i):
+            exp_of_v = ring2.tile([P, PACK, P], F32, name="exp_of_v")
+            nc.scalar.activation(
+                out=exp_of_v[:], in_=live["v_plus1", i][:], func=ACT.Exp, bias=-1.0
+            )
+            live["exp_of_v", i] = exp_of_v
+
+        def elu_and_transpose(i):
+            d_plus1 = ring2.tile([P, PACK, P], F32, name="d_plus1")
+            nc.vector.scalar_tensor_tensor(
+                out=d_plus1[:],
+                in0=live.pop(("exp_of_v", i))[:],
+                scalar=1.0,
+                in1=live.pop(("v_plus1", i))[:],
+                op0=ALU.min,
+                op1=ALU.max,
+            )
+            d_t = banks.tile([P, PACK, P], F32, name="d_t")
+            for t in range(PACK):
+                nc.tensor.transpose(d_t[:, t, :], d_plus1[:, t, :], ident[:])
+            live["d_t", i] = d_t
+
+        def copy_d(i):
+            d_grouped = ring3.tile([P, P, PACK], BF16, align_bytes=64, name="d_grouped")
+            nc.scalar.activation(
+                out=d_grouped[:],
+                in_=live.pop(("d_t", i))[:].rearrange("p t r -> p r t"),
+                func=ACT.Identity,
+                bias=-1.0,
+            )
+            live["d_grouped", i] = d_grouped
+
+        def logit_matmuls(i):
+            codes = ring3.tile([P, P], U32, align_bytes=64, name="d_codes")
+            scales = ring3.tile([P, P], U8, align_bytes=64, name="d_scales")
+            nc.vector.quantize_mx(
+                out=codes[:].bitcast(FP8X4),
+                scales=scales[:],
+                in_=live.pop(("d_grouped", i))[:].rearrange("p r t -> p (r t)"),
+            )
             for c in range(HALVES):
-                acc = banks.tile([P, BANK], F32, tag="bank", name="acc2")
+                acc = banks.tile([P, BANK], F32, name="acc2")
                 nc.tensor.matmul_mx(
                     out=acc[:],
-                    lhsT=d_codes[:, cols].bitcast(FP8X4),
-                    lhsT_scale=d_scales[:, cols],
+                    lhsT=codes[:].bitcast(FP8X4),
+                    lhsT_scale=scales[:],
                     rhs=w3[:, c * 2 * BANK : (c + 1) * 2 * BANK].bitcast(FP4X4),
                     rhs_scale=planes[:, HIDDEN + c * BANK : HIDDEN + (c + 1) * BANK],
                     start=True,
                     stop=True,
                 )
+                live["acc2", i, c] = acc
+
+        def add_bias3(i):
+            logit = logit_pool.tile([P, PIXELS], F32, name="logit")
+            for c in range(HALVES):
                 nc.vector.tensor_tensor(
                     out=logit[:, c * BANK : (c + 1) * BANK],
-                    in0=acc[:],
+                    in0=live.pop(("acc2", i, c))[:],
                     in1=b3_rows[:, c * BANK : (c + 1) * BANK],
                     op=ALU.add,
                 )
-            logit_tiles[i] = logit
+            live["logit", i] = logit
 
-        def absolute(i):
-            logit = logit_tiles[i]
-            abs_l = group_pool.tile([P, PIXELS], F32, name="abs_l")
+        def abs_on_vector(i):
+            logit = live["logit", i]
+            abs_l = abs_pool.tile([P, PIXELS], F32, name="abs_l")
             nc.vector.scalar_tensor_tensor(
                 out=abs_l[:, ABS_ON_SCALAR:],
                 in0=logit[:, ABS_ON_SCALAR:],
@@ -261,19 +253,22 @@ def tile_gmvae_pb_kernel(
                 op1=ALU.max,
                 accum_out=sum_abs_vector[:, i : i + 1],
             )
+            live["abs_l", i] = abs_l
+
+        def abs_on_scalar(i):
             nc.scalar.activation(
-                out=abs_l[:, :ABS_ON_SCALAR],
-                in_=logit[:, :ABS_ON_SCALAR],
+                out=live["abs_l", i][:, :ABS_ON_SCALAR],
+                in_=live["logit", i][:, :ABS_ON_SCALAR],
                 func=ACT.Abs,
                 accum_out=sum_abs_scalar[:, i : i + 1],
             )
-            abs_tiles[i] = abs_l
 
         def exp_minus_abs(i):
-            nc.scalar.activation(out=abs_tiles[i][:], in_=abs_tiles[i][:], func=ACT.Exp, scale=-1.0)
+            abs_l = live["abs_l", i]
+            nc.scalar.activation(out=abs_l[:], in_=abs_l[:], func=ACT.Exp, scale=-1.0)
 
         def dot_with_x(i):
-            logit = logit_tiles.pop(i)
+            logit = live.pop(("logit", i))
             nc.vector.scalar_tensor_tensor(
                 out=logit[:],
                 in0=x_loads[i // LOAD_TILES][:, i % LOAD_TILES, :],
@@ -285,22 +280,34 @@ def tile_gmvae_pb_kernel(
             )
 
         def log1p(i):
-            e = abs_tiles.pop(i)
+            e = live.pop(("abs_l", i))
             nc.scalar.activation(
                 out=e[:], in_=e[:], func=ACT.Ln, bias=1.0, accum_out=sum_log[:, i : i + 1]
             )
 
-        for first in range(0, N_TILES, GROUP):
-            for n in range(GROUP + 2):
-                if n < GROUP:
-                    logits(first + n)
-                if 1 <= n <= GROUP:
-                    absolute(first + n - 1)
-                if n >= 2:
-                    exp_minus_abs(first + n - 2)
-            for i in range(first, first + GROUP):
-                dot_with_x(i)
-                log1p(i)
+        def run(step, i, count=N_TILES):
+            if 0 <= i < count:
+                step(i)
+
+        for n in range(N_TILES + LAG_EXP_ABS):
+            run(logit_matmuls, n - LAG_LOGITS)
+            run(quantise_h, n - LAG_QUANT_H, N_PAIRS)
+            run(hidden_matmul, n - LAG_HIDDEN)
+            run(copy_d, n - LAG_COPY_D)
+            run(elu_and_transpose, n - LAG_ELU)
+            run(copy_h, n - LAG_COPY_H, N_PAIRS)
+            run(abs_on_vector, n - LAG_ABS)
+            run(exp_v, n - LAG_EXP)
+            run(add_bias2, n - LAG_HIDDEN)
+            run(abs_on_scalar, n - LAG_ABS)
+            run(add_bias3, n - LAG_LOGITS)
+            run(exp_minus_abs, n - LAG_EXP_ABS)
+            run(transpose_h, n, N_PAIRS)
+            done = n - LAG_EXP_ABS + 1
+            if done > 0 and done % GROUP == 0:
+                for i in range(done - GROUP, done):
+                    dot_with_x(i)
+                    log1p(i)
 
         sum_abs = keep.tile([P, N_TILES], F32)
         nc.vector.tensor_tensor(

@@ -23,19 +23,21 @@ PAIR = 2
 N_PAIRS = N_TILES // PAIR
 LOAD_TILES = 4
 GROUP = 12
-ABS_ON_SCALAR = 576
+ABS_ON_SCALAR = 512
 
 FLOPS = 2 * BATCH * HIDDEN * (HIDDEN + PIXELS)
 
 LAG_COPY_H = 1
 LAG_QUANT_H = 2
 LAG_HIDDEN = 2
-LAG_EXP = 3
-LAG_ELU = 4
-LAG_COPY_D = 5
-LAG_LOGITS = 6
-LAG_ABS = 7
-LAG_EXP_ABS = 8
+LAG_BIAS2 = 3
+LAG_EXP = 4
+LAG_ELU = 5
+LAG_COPY_D = 6
+LAG_LOGITS = 7
+LAG_BIAS3 = 8
+LAG_ABS = 9
+LAG_EXP_ABS = 10
 
 
 def tile_gmvae_pb_kernel(
@@ -51,12 +53,14 @@ def tile_gmvae_pb_kernel(
         ring2 = stack.enter_context(tc.tile_pool(name="ring2", bufs=2))
         ring3 = stack.enter_context(tc.tile_pool(name="ring3", bufs=3))
         logit_pool = stack.enter_context(
-            tc.tile_pool(name="logit", bufs=GROUP + LAG_EXP_ABS - LAG_LOGITS)
+            tc.tile_pool(name="logit", bufs=GROUP + LAG_EXP_ABS - LAG_BIAS3)
         )
         abs_pool = stack.enter_context(
             tc.tile_pool(name="abs", bufs=GROUP + LAG_EXP_ABS - LAG_ABS)
         )
-        banks = stack.enter_context(tc.psum_pool(name="banks", bufs=2))
+        banks_t = stack.enter_context(tc.psum_pool(name="banks_t", bufs=1))
+        banks_1 = stack.enter_context(tc.psum_pool(name="banks_1", bufs=2))
+        banks_2 = stack.enter_context(tc.psum_pool(name="banks_2", bufs=2 * HALVES))
 
         planes = keep.tile([P, HIDDEN + PIXELS], U8, align_bytes=64)
         planes_i32 = planes[:].bitcast(I32)
@@ -130,7 +134,7 @@ def tile_gmvae_pb_kernel(
         h_scales = keep.tile([P, BATCH], U8, align_bytes=64)
 
         def transpose_h(j):
-            h_t = banks.tile([P, PAIR, 2, P], F32, name="h_t")
+            h_t = banks_t.tile([P, PAIR, 2, P], F32, name="h_t")
             for s in range(PAIR):
                 words = h_loads[j][:, s, :].bitcast(F32)
                 for u in range(2):
@@ -155,7 +159,7 @@ def tile_gmvae_pb_kernel(
 
         def hidden_matmul(i):
             cols = slice(i * P, (i + 1) * P)
-            acc = banks.tile([P, BANK], F32, name="acc1")
+            acc = banks_1.tile([P, BANK], F32, name="acc1")
             nc.tensor.matmul_mx(
                 out=acc[:],
                 lhsT=h_codes[:, cols].bitcast(FP8X4),
@@ -194,7 +198,7 @@ def tile_gmvae_pb_kernel(
                 op0=ALU.min,
                 op1=ALU.max,
             )
-            d_t = banks.tile([P, PACK, P], F32, name="d_t")
+            d_t = banks_t.tile([P, PACK, P], F32, name="d_t")
             for t in range(PACK):
                 nc.tensor.transpose(d_t[:, t, :], d_plus1[:, t, :], ident[:])
             live["d_t", i] = d_t
@@ -218,7 +222,7 @@ def tile_gmvae_pb_kernel(
                 in_=live.pop(("d_grouped", i))[:].rearrange("p r t -> p (r t)"),
             )
             for c in range(HALVES):
-                acc = banks.tile([P, BANK], F32, name="acc2")
+                acc = banks_2.tile([P, BANK], F32, name="acc2")
                 nc.tensor.matmul_mx(
                     out=acc[:],
                     lhsT=codes[:].bitcast(FP8X4),
@@ -241,9 +245,9 @@ def tile_gmvae_pb_kernel(
                 )
             live["logit", i] = logit
 
-        def abs_on_vector(i):
+        def abs_on_vector_part(i):
             logit = live["logit", i]
-            abs_l = abs_pool.tile([P, PIXELS], F32, name="abs_l")
+            abs_l = live["abs_l", i]
             nc.vector.scalar_tensor_tensor(
                 out=abs_l[:, ABS_ON_SCALAR:],
                 in0=logit[:, ABS_ON_SCALAR:],
@@ -253,9 +257,9 @@ def tile_gmvae_pb_kernel(
                 op1=ALU.max,
                 accum_out=sum_abs_vector[:, i : i + 1],
             )
-            live["abs_l", i] = abs_l
 
         def abs_on_scalar(i):
+            live["abs_l", i] = abs_pool.tile([P, PIXELS], F32, name="abs_l")
             nc.scalar.activation(
                 out=live["abs_l", i][:, :ABS_ON_SCALAR],
                 in_=live["logit", i][:, :ABS_ON_SCALAR],
@@ -296,11 +300,11 @@ def tile_gmvae_pb_kernel(
             run(copy_d, n - LAG_COPY_D)
             run(elu_and_transpose, n - LAG_ELU)
             run(copy_h, n - LAG_COPY_H, N_PAIRS)
-            run(abs_on_vector, n - LAG_ABS)
+            run(add_bias2, n - LAG_BIAS2)
             run(exp_v, n - LAG_EXP)
-            run(add_bias2, n - LAG_HIDDEN)
+            run(add_bias3, n - LAG_BIAS3)
             run(abs_on_scalar, n - LAG_ABS)
-            run(add_bias3, n - LAG_LOGITS)
+            run(abs_on_vector_part, n - LAG_ABS)
             run(exp_minus_abs, n - LAG_EXP_ABS)
             run(transpose_h, n, N_PAIRS)
             done = n - LAG_EXP_ABS + 1

@@ -19,16 +19,14 @@ BATCH, HIDDEN, PIXELS = 3072, 512, 1024
 N_TILES = BATCH // P
 BANK = 512
 HALVES = PIXELS // BANK
-PAIR = 2
-N_PAIRS = N_TILES // PAIR
-LOAD_TILES = 4
+H_LOAD_TILES = 2
+X_LOAD_TILES = 4
 GROUP = 12
-ABS_ON_SCALAR = 512
+ABS_ON_SCALAR = 448
 
 FLOPS = 2 * BATCH * HIDDEN * (HIDDEN + PIXELS)
 
 LAG_COPY_H = 1
-LAG_QUANT_H = 2
 LAG_HIDDEN = 2
 LAG_BIAS2 = 3
 LAG_EXP = 4
@@ -69,11 +67,11 @@ def tile_gmvae_pb_kernel(
         make_identity(nc, ident[:])
 
         h_loads = []
-        for j in range(N_PAIRS):
-            h_loads.append(keep.tile([P, PAIR, HIDDEN], BF16, name="h_load%d" % j))
+        for c in range(N_TILES // H_LOAD_TILES):
+            h_loads.append(keep.tile([P, H_LOAD_TILES, HIDDEN], BF16, name="h_load%d" % c))
         x_loads = []
-        for c in range(N_TILES // LOAD_TILES):
-            x_loads.append(keep.tile([P, LOAD_TILES, PIXELS], BF16, name="x_load%d" % c))
+        for c in range(N_TILES // X_LOAD_TILES):
+            x_loads.append(keep.tile([P, X_LOAD_TILES, PIXELS], BF16, name="x_load%d" % c))
         w2 = keep.tile([P, 2 * HIDDEN], U8, align_bytes=64)
         w3 = keep.tile([P, 2 * PIXELS], U8, align_bytes=64)
         b2_rows = keep.tile([P, HIDDEN], BF16)
@@ -88,8 +86,10 @@ def tile_gmvae_pb_kernel(
                     in_=rows[r:16:4, :],
                 )
 
-        def load_h(j):
-            nc.sync.dma_start(out=h_loads[j][:], in_=h_rows[:, j * PAIR : (j + 1) * PAIR, :])
+        def load_h(c):
+            nc.sync.dma_start(
+                out=h_loads[c][:], in_=h_rows[:, c * H_LOAD_TILES : (c + 1) * H_LOAD_TILES, :]
+            )
 
         nc.scalar.dma_start(out=b2_rows[:], in_=db2.partition_broadcast(P))
         load_h(0)
@@ -97,18 +97,18 @@ def tile_gmvae_pb_kernel(
             out=w2[:].bitcast(I32), in_=dw2_words.rearrange("g p n -> (g p) n").bitcast(I32)
         )
         load_scales(dw2_scales, 0)
-        for j in range(1, 4):
-            load_h(j)
+        for c in range(1, 3):
+            load_h(c)
         nc.sync.dma_start(
             out=w3[:].bitcast(I32), in_=dw3_words.rearrange("g p n -> (g p) n").bitcast(I32)
         )
         load_scales(dw3_scales, HIDDEN)
         nc.sync.dma_start(out=b3_rows[:], in_=db3.partition_broadcast(P))
-        for j in range(4, N_PAIRS):
-            load_h(j)
-        for c in range(N_TILES // LOAD_TILES):
+        for c in range(3, N_TILES // H_LOAD_TILES):
+            load_h(c)
+        for c in range(N_TILES // X_LOAD_TILES):
             nc.sync.dma_start(
-                out=x_loads[c][:], in_=x_rows[:, c * LOAD_TILES : (c + 1) * LOAD_TILES, :]
+                out=x_loads[c][:], in_=x_rows[:, c * X_LOAD_TILES : (c + 1) * X_LOAD_TILES, :]
             )
 
         warm = keep.tile([P, 2], F32)
@@ -130,40 +130,34 @@ def tile_gmvae_pb_kernel(
         sum_log = keep.tile([P, N_TILES], F32)
         live = {}
 
-        h_codes = keep.tile([P, BATCH], U32, align_bytes=64)
-        h_scales = keep.tile([P, BATCH], U8, align_bytes=64)
+        def transpose_h(i):
+            words = h_loads[i // H_LOAD_TILES][:, i % H_LOAD_TILES, :].bitcast(F32)
+            h_t = banks_t.tile([P, 2, P], F32, name="h_t")
+            for u in range(2):
+                nc.tensor.transpose(h_t[:, u, :], words[:, u : HIDDEN // 2 : 2], ident[:])
+            live["h_t", i] = h_t
 
-        def transpose_h(j):
-            h_t = banks_t.tile([P, PAIR, 2, P], F32, name="h_t")
-            for s in range(PAIR):
-                words = h_loads[j][:, s, :].bitcast(F32)
-                for u in range(2):
-                    nc.tensor.transpose(h_t[:, s, u, :], words[:, u : HIDDEN // 2 : 2], ident[:])
-            live["h_t", j] = h_t
-
-        def copy_h(j):
-            h_grouped = ring2.tile([P, PAIR * P * PACK], BF16, align_bytes=64, name="h_grouped")
+        def copy_h(i):
+            h_grouped = ring2.tile([P, P * PACK], BF16, align_bytes=64, name="h_grouped")
             nc.scalar.copy(
-                out=h_grouped[:].bitcast(F32).rearrange("p (s r u) -> p s r u", s=PAIR, u=2),
-                in_=live.pop(("h_t", j))[:].rearrange("p s u r -> p s r u"),
+                out=h_grouped[:].bitcast(F32).rearrange("p (r u) -> p r u", u=2),
+                in_=live.pop(("h_t", i))[:].rearrange("p u r -> p r u"),
             )
-            live["h_grouped", j] = h_grouped
-
-        def quantise_h(j):
-            cols = slice(j * PAIR * P, (j + 1) * PAIR * P)
-            nc.vector.quantize_mx(
-                out=h_codes[:, cols].bitcast(FP8X4),
-                scales=h_scales[:, cols],
-                in_=live.pop(("h_grouped", j))[:],
-            )
+            live["h_grouped", i] = h_grouped
 
         def hidden_matmul(i):
-            cols = slice(i * P, (i + 1) * P)
+            codes = ring3.tile([P, P], U32, align_bytes=64, name="h_codes")
+            scales = ring3.tile([P, P], U8, align_bytes=64, name="h_scales")
+            nc.vector.quantize_mx(
+                out=codes[:].bitcast(FP8X4),
+                scales=scales[:],
+                in_=live.pop(("h_grouped", i))[:],
+            )
             acc = banks_1.tile([P, BANK], F32, name="acc1")
             nc.tensor.matmul_mx(
                 out=acc[:],
-                lhsT=h_codes[:, cols].bitcast(FP8X4),
-                lhsT_scale=h_scales[:, cols],
+                lhsT=codes[:].bitcast(FP8X4),
+                lhsT_scale=scales[:],
                 rhs=w2[:].bitcast(FP4X4),
                 rhs_scale=planes[:, 0:HIDDEN],
                 start=True,
@@ -275,7 +269,7 @@ def tile_gmvae_pb_kernel(
             logit = live.pop(("logit", i))
             nc.vector.scalar_tensor_tensor(
                 out=logit[:],
-                in0=x_loads[i // LOAD_TILES][:, i % LOAD_TILES, :],
+                in0=x_loads[i // X_LOAD_TILES][:, i % X_LOAD_TILES, :],
                 scalar=-0.5,
                 in1=logit[:],
                 op0=ALU.add,
@@ -289,24 +283,23 @@ def tile_gmvae_pb_kernel(
                 out=e[:], in_=e[:], func=ACT.Ln, bias=1.0, accum_out=sum_log[:, i : i + 1]
             )
 
-        def run(step, i, count=N_TILES):
-            if 0 <= i < count:
+        def run(step, i):
+            if 0 <= i < N_TILES:
                 step(i)
 
         for n in range(N_TILES + LAG_EXP_ABS):
             run(logit_matmuls, n - LAG_LOGITS)
-            run(quantise_h, n - LAG_QUANT_H, N_PAIRS)
             run(hidden_matmul, n - LAG_HIDDEN)
             run(copy_d, n - LAG_COPY_D)
             run(elu_and_transpose, n - LAG_ELU)
-            run(copy_h, n - LAG_COPY_H, N_PAIRS)
+            run(copy_h, n - LAG_COPY_H)
             run(add_bias2, n - LAG_BIAS2)
             run(exp_v, n - LAG_EXP)
             run(add_bias3, n - LAG_BIAS3)
             run(abs_on_scalar, n - LAG_ABS)
             run(abs_on_vector_part, n - LAG_ABS)
             run(exp_minus_abs, n - LAG_EXP_ABS)
-            run(transpose_h, n, N_PAIRS)
+            run(transpose_h, n)
             done = n - LAG_EXP_ABS + 1
             if done > 0 and done % GROUP == 0:
                 for i in range(done - GROUP, done):

@@ -19,23 +19,24 @@ BATCH, HIDDEN, PIXELS = 3072, 512, 1024
 N_TILES = BATCH // P
 BANK = 512
 HALVES = PIXELS // BANK
-H_LOAD_TILES = 2
-X_LOAD_TILES = 4
-GROUP = 12
-ABS_ON_SCALAR = 448
+PAIR = 2
+N_PAIRS = N_TILES // PAIR
+QUADS = [(0,), (1,)] + [(m, m + 1) for m in range(2, N_PAIRS, 2)]
+GROUP = 6
+COPY_ON_SCALAR = (0, 1, 2, 3, 4, 5)
+RELU_ON_VECTOR = (0,)
+ABS0_ON_VECTOR = (5, 6, 7, 8)
+ABS1_ON_VECTOR = tuple(range(N_PAIRS))
+PREP = [[2, 3], [4, 5], [6, 7], [8], [9], [10], [11], [], [], [], [], []]
+STEPS = [4, 4, 4, 2, 2, 2, 2, 0, 2, 2, 0, 0]
+DOTS = [0, 0, 0, 0, 0, 0, 0, 2, 2, 2, 2]
+LOGIT_BUFS = 9
+ABS_BUFS = 7
+ER_BUFS = 2
+H_AHEAD = 6
+X_AHEAD = 7
 
 FLOPS = 2 * BATCH * HIDDEN * (HIDDEN + PIXELS)
-
-LAG_COPY_H = 1
-LAG_HIDDEN = 2
-LAG_BIAS2 = 3
-LAG_EXP = 4
-LAG_ELU = 5
-LAG_COPY_D = 6
-LAG_LOGITS = 7
-LAG_BIAS3 = 8
-LAG_ABS = 9
-LAG_EXP_ABS = 10
 
 
 def tile_gmvae_pb_kernel(
@@ -48,268 +49,328 @@ def tile_gmvae_pb_kernel(
     with ExitStack() as stack:
         stack.enter_context(tc.manual_schedule())
         keep = stack.enter_context(tc.tile_pool(name="keep", bufs=1))
+        h_pool = stack.enter_context(tc.tile_pool(name="h", bufs=H_AHEAD))
+        x_pool = stack.enter_context(tc.tile_pool(name="x", bufs=X_AHEAD))
         ring2 = stack.enter_context(tc.tile_pool(name="ring2", bufs=2))
-        ring3 = stack.enter_context(tc.tile_pool(name="ring3", bufs=3))
-        logit_pool = stack.enter_context(
-            tc.tile_pool(name="logit", bufs=GROUP + LAG_EXP_ABS - LAG_BIAS3)
-        )
-        abs_pool = stack.enter_context(
-            tc.tile_pool(name="abs", bufs=GROUP + LAG_EXP_ABS - LAG_ABS)
-        )
-        banks_t = stack.enter_context(tc.psum_pool(name="banks_t", bufs=1))
+        logit_pool = stack.enter_context(tc.tile_pool(name="logit", bufs=LOGIT_BUFS))
+        abs_pool = stack.enter_context(tc.tile_pool(name="abs", bufs=ABS_BUFS))
+        er_pool = stack.enter_context(tc.tile_pool(name="er", bufs=ER_BUFS))
+        banks_t = stack.enter_context(tc.psum_pool(name="banks_t", bufs=2))
         banks_1 = stack.enter_context(tc.psum_pool(name="banks_1", bufs=2))
         banks_2 = stack.enter_context(tc.psum_pool(name="banks_2", bufs=2 * HALVES))
 
-        planes = keep.tile([P, HIDDEN + PIXELS], U8, align_bytes=64)
-        planes_i32 = planes[:].bitcast(I32)
-        nc.vector.memset(planes_i32, 0)
+        planes2_raw = keep.tile([P, HIDDEN], U8, align_bytes=64)
+        planes3 = keep.tile([P, PIXELS], U8, align_bytes=64)
+        nc.vector.memset(planes2_raw[:].bitcast(I32), 0)
+        nc.vector.memset(planes3[:].bitcast(I32), 0)
         ident = keep.tile([P, P], F32)
         make_identity(nc, ident[:])
 
-        h_loads = []
-        for c in range(N_TILES // H_LOAD_TILES):
-            h_loads.append(keep.tile([P, H_LOAD_TILES, HIDDEN], BF16, name="h_load%d" % c))
-        x_loads = []
-        for c in range(N_TILES // X_LOAD_TILES):
-            x_loads.append(keep.tile([P, X_LOAD_TILES, PIXELS], BF16, name="x_load%d" % c))
-        w2 = keep.tile([P, 2 * HIDDEN], U8, align_bytes=64)
+        live = {}
+
+        w2_raw = keep.tile([P, 2 * HIDDEN], U8, align_bytes=64)
+        w2 = keep.tile([P, PACK, 2 * P], U8, align_bytes=64)
+        planes2 = keep.tile([P, PACK, P], U8, align_bytes=64)
         w3 = keep.tile([P, 2 * PIXELS], U8, align_bytes=64)
-        b2_rows = keep.tile([P, HIDDEN], BF16)
+        b2_raw = keep.tile([P, PACK], BF16)
+        b2 = keep.tile([P, PACK], F32)
         b3_rows = keep.tile([P, PIXELS], BF16)
 
-        def load_scales(scales, first_col):
+        def load_scales(scales, planes):
             rows = scales.rearrange("g q n -> (g q) n").bitcast(I32)
-            width = rows.shape[1]
             for r in range(4):
-                nc.sync.dma_start(
-                    out=planes_i32[r:P:32, first_col // 4 : first_col // 4 + width],
-                    in_=rows[r:16:4, :],
-                )
+                nc.sync.dma_start(out=planes[:].bitcast(I32)[r:P:32, :], in_=rows[r:16:4, :])
 
-        def load_h(c):
-            nc.sync.dma_start(
-                out=h_loads[c][:], in_=h_rows[:, c * H_LOAD_TILES : (c + 1) * H_LOAD_TILES, :]
-            )
+        def load_h(m):
+            live["h", m] = h_pool.tile([P, PAIR, HIDDEN], BF16, name="h_load")
+            nc.sync.dma_start(out=live["h", m][:], in_=h_rows[:, m * PAIR : (m + 1) * PAIR, :])
 
-        nc.scalar.dma_start(out=b2_rows[:], in_=db2.partition_broadcast(P))
+        def load_x(m):
+            live["x", m] = x_pool.tile([P, PAIR, PIXELS], BF16, name="x_load")
+            nc.sync.dma_start(out=live["x", m][:], in_=x_rows[:, m * PAIR : (m + 1) * PAIR, :])
+
+        nc.scalar.dma_start(out=b2_raw[:], in_=db2.rearrange("(p t) -> p t", t=PACK))
         load_h(0)
         nc.sync.dma_start(
-            out=w2[:].bitcast(I32), in_=dw2_words.rearrange("g p n -> (g p) n").bitcast(I32)
+            out=w2_raw[:].bitcast(I32), in_=dw2_words.rearrange("g p n -> (g p) n").bitcast(I32)
         )
-        load_scales(dw2_scales, 0)
-        for c in range(1, 3):
-            load_h(c)
+        load_scales(dw2_scales, planes2_raw)
+        for m in range(1, 4):
+            load_h(m)
         nc.sync.dma_start(
             out=w3[:].bitcast(I32), in_=dw3_words.rearrange("g p n -> (g p) n").bitcast(I32)
         )
-        load_scales(dw3_scales, HIDDEN)
+        load_scales(dw3_scales, planes3)
         nc.sync.dma_start(out=b3_rows[:], in_=db3.partition_broadcast(P))
-        for c in range(3, N_TILES // H_LOAD_TILES):
-            load_h(c)
-        for c in range(N_TILES // X_LOAD_TILES):
-            nc.sync.dma_start(
-                out=x_loads[c][:], in_=x_rows[:, c * X_LOAD_TILES : (c + 1) * X_LOAD_TILES, :]
-            )
+        for m in range(4, H_AHEAD):
+            load_h(m)
+        for m in range(X_AHEAD):
+            load_x(m)
 
         warm = keep.tile([P, 2], F32)
         nc.vector.memset(warm[:], 0.0)
         nc.scalar.activation(out=warm[:, 1:2], in_=warm[:, 0:1], func=ACT.Exp)
 
-        b2_plus1 = keep.tile([P, PACK, P], F32)
-        nc.vector.tensor_scalar(
-            out=b2_plus1[:],
-            in0=b2_rows[:].rearrange("p (q t) -> p t q", t=PACK),
-            scalar1=1.0,
-            scalar2=None,
-            op0=ALU.add,
+        nc.vector.tensor_copy(
+            out=w2[:].rearrange("p t (m b) -> p t m b", b=2),
+            in_=w2_raw[:].rearrange("p (m t b) -> p t m b", t=PACK, b=2),
         )
+        nc.vector.tensor_copy(
+            out=planes2[:], in_=planes2_raw[:].rearrange("p (m t) -> p t m", t=PACK)
+        )
+        nc.vector.tensor_copy(out=b2[:], in_=b2_raw[:])
 
         sum_xl = keep.tile([P, N_TILES], F32)
-        sum_abs_vector = keep.tile([P, N_TILES], F32)
-        sum_abs_scalar = keep.tile([P, N_TILES], F32)
+        sum_abs = keep.tile([P, N_TILES], F32)
         sum_log = keep.tile([P, N_TILES], F32)
-        live = {}
+        def transpose_h(m):
+            words = live.pop(("h", m))[:].bitcast(F32)
+            h_t = banks_t.tile([P, PAIR, 2, P], F32, name="h_t")
+            for j in range(PAIR):
+                for u in range(2):
+                    nc.tensor.transpose(
+                        h_t[:, j, u, :], words[:, j, u : HIDDEN // 2 : 2], ident[:]
+                    )
+            live["h_t", m] = h_t
+            if m + H_AHEAD < N_PAIRS:
+                load_h(m + H_AHEAD)
 
-        def transpose_h(i):
-            words = h_loads[i // H_LOAD_TILES][:, i % H_LOAD_TILES, :].bitcast(F32)
-            h_t = banks_t.tile([P, 2, P], F32, name="h_t")
-            for u in range(2):
-                nc.tensor.transpose(h_t[:, u, :], words[:, u : HIDDEN // 2 : 2], ident[:])
-            live["h_t", i] = h_t
+        def copy_h(m):
+            h_grouped = ring2.tile([P, PAIR * P * PACK], BF16, align_bytes=64, name="h_grouped")
+            out = h_grouped[:].bitcast(F32).rearrange("p (j r u) -> p j r u", j=PAIR, u=2)
+            in_ = live.pop(("h_t", m))[:].rearrange("p j u r -> p j r u")
+            if m in COPY_ON_SCALAR:
+                nc.scalar.copy(out=out, in_=in_)
+            else:
+                nc.vector.tensor_copy(out=out, in_=in_)
+            live["h_grouped", m] = h_grouped
 
-        def copy_h(i):
-            h_grouped = ring2.tile([P, P * PACK], BF16, align_bytes=64, name="h_grouped")
-            nc.scalar.copy(
-                out=h_grouped[:].bitcast(F32).rearrange("p (r u) -> p r u", u=2),
-                in_=live.pop(("h_t", i))[:].rearrange("p u r -> p r u"),
-            )
-            live["h_grouped", i] = h_grouped
+        def place(m):
+            for q, pairs in enumerate(QUADS):
+                if m in pairs:
+                    first = pairs.index(m) * PAIR * P
+                    return q, slice(first, first + PAIR * P)
 
-        def hidden_matmul(i):
-            codes = ring3.tile([P, P], U32, align_bytes=64, name="h_codes")
-            scales = ring3.tile([P, P], U8, align_bytes=64, name="h_scales")
+        def quantize_h(m):
+            q, cols = place(m)
+            if m == QUADS[q][0]:
+                live["h_codes", q] = ring2.tile([P, BANK], U32, align_bytes=64, name="h_codes")
+                live["h_scales", q] = ring2.tile([P, BANK], U8, align_bytes=64, name="h_scales")
             nc.vector.quantize_mx(
-                out=codes[:].bitcast(FP8X4),
-                scales=scales[:],
-                in_=live.pop(("h_grouped", i))[:],
+                out=live["h_codes", q][:, cols].bitcast(FP8X4),
+                scales=live["h_scales", q][:, cols],
+                in_=live.pop(("h_grouped", m))[:],
             )
-            acc = banks_1.tile([P, BANK], F32, name="acc1")
+
+        def hidden_matmul(q, t):
+            width = len(QUADS[q]) * PAIR * P
+            acc = banks_1.tile([P, BANK], F32, name="acc1") if q else banks_2.tile([P, BANK], F32, name="acc2")
             nc.tensor.matmul_mx(
-                out=acc[:],
-                lhsT=codes[:].bitcast(FP8X4),
-                lhsT_scale=scales[:],
-                rhs=w2[:].bitcast(FP4X4),
-                rhs_scale=planes[:, 0:HIDDEN],
+                out=acc[:, :width],
+                lhsT=w2[:, t, :].bitcast(FP4X4),
+                lhsT_scale=planes2[:, t, :],
+                rhs=live["h_codes", q][:, :width].bitcast(FP8X4),
+                rhs_scale=live["h_scales", q][:, :width],
                 start=True,
                 stop=True,
             )
-            live["acc1", i] = acc
+            live["acc1", q, t] = acc
 
-        def add_bias2(i):
-            v_plus1 = ring3.tile([P, PACK, P], F32, name="v_plus1")
-            nc.vector.tensor_tensor(
-                out=v_plus1[:],
-                in0=live.pop(("acc1", i))[:].rearrange("p (q t) -> p t q", t=PACK),
-                in1=b2_plus1[:],
-                op=ALU.add,
-            )
-            live["v_plus1", i] = v_plus1
-
-        def exp_v(i):
-            exp_of_v = ring2.tile([P, PACK, P], F32, name="exp_of_v")
+        def exp_and_relu(q, t):
+            width = len(QUADS[q]) * PAIR * P
+            if t == 0:
+                live["exp_v", q] = er_pool.tile([P, PACK, BANK], F32, name="exp_v")
+                live["relu_v", q] = er_pool.tile([P, PACK, BANK], F32, name="relu_v")
+            acc = live.pop(("acc1", q, t))
             nc.scalar.activation(
-                out=exp_of_v[:], in_=live["v_plus1", i][:], func=ACT.Exp, bias=-1.0
+                out=live["exp_v", q][:, t, :width],
+                in_=acc[:, :width],
+                func=ACT.Exp,
+                bias=b2[:, t : t + 1],
             )
-            live["exp_of_v", i] = exp_of_v
+            if q in RELU_ON_VECTOR or (q, t) in RELU_ON_VECTOR:
+                nc.vector.tensor_scalar(
+                    out=live["relu_v", q][:, t, :width],
+                    in0=acc[:, :width],
+                    scalar1=b2[:, t : t + 1],
+                    scalar2=0.0,
+                    op0=ALU.add,
+                    op1=ALU.max,
+                )
+            else:
+                nc.scalar.activation(
+                    out=live["relu_v", q][:, t, :width],
+                    in_=acc[:, :width],
+                    func=ACT.Relu,
+                    bias=b2[:, t : t + 1],
+                )
 
-        def elu_and_transpose(i):
-            d_plus1 = ring2.tile([P, PACK, P], F32, name="d_plus1")
+        def elu(m):
+            q, cols = place(m)
+            d_grouped = ring2.tile([P, PAIR * P, PACK], BF16, align_bytes=64, name="d_grouped")
             nc.vector.scalar_tensor_tensor(
-                out=d_plus1[:],
-                in0=live.pop(("exp_of_v", i))[:],
-                scalar=1.0,
-                in1=live.pop(("v_plus1", i))[:],
-                op0=ALU.min,
-                op1=ALU.max,
-            )
-            d_t = banks_t.tile([P, PACK, P], F32, name="d_t")
-            for t in range(PACK):
-                nc.tensor.transpose(d_t[:, t, :], d_plus1[:, t, :], ident[:])
-            live["d_t", i] = d_t
-
-        def copy_d(i):
-            d_grouped = ring3.tile([P, P, PACK], BF16, align_bytes=64, name="d_grouped")
-            nc.scalar.activation(
                 out=d_grouped[:],
-                in_=live.pop(("d_t", i))[:].rearrange("p t r -> p r t"),
-                func=ACT.Identity,
-                bias=-1.0,
+                in0=live["exp_v", q][:, :, cols].rearrange("p t r -> p r t"),
+                scalar=-1.0,
+                in1=live["relu_v", q][:, :, cols].rearrange("p t r -> p r t"),
+                op0=ALU.add,
+                op1=ALU.min,
             )
-            live["d_grouped", i] = d_grouped
+            live["d_grouped", m] = d_grouped
 
-        def logit_matmuls(i):
-            codes = ring3.tile([P, P], U32, align_bytes=64, name="d_codes")
-            scales = ring3.tile([P, P], U8, align_bytes=64, name="d_scales")
+        def logit_matmuls(m):
+            codes = ring2.tile([P, PAIR * P], U32, align_bytes=64, name="d_codes")
+            scales = ring2.tile([P, PAIR * P], U8, align_bytes=64, name="d_scales")
             nc.vector.quantize_mx(
                 out=codes[:].bitcast(FP8X4),
                 scales=scales[:],
-                in_=live.pop(("d_grouped", i))[:].rearrange("p r t -> p (r t)"),
+                in_=live.pop(("d_grouped", m))[:].rearrange("p r t -> p (r t)"),
             )
-            for c in range(HALVES):
-                acc = banks_2.tile([P, BANK], F32, name="acc2")
-                nc.tensor.matmul_mx(
-                    out=acc[:],
-                    lhsT=codes[:].bitcast(FP8X4),
-                    lhsT_scale=scales[:],
-                    rhs=w3[:, c * 2 * BANK : (c + 1) * 2 * BANK].bitcast(FP4X4),
-                    rhs_scale=planes[:, HIDDEN + c * BANK : HIDDEN + (c + 1) * BANK],
-                    start=True,
-                    stop=True,
+            for j in range(PAIR):
+                rows = slice(j * P, (j + 1) * P)
+                for c in range(HALVES):
+                    acc = banks_2.tile([P, BANK], F32, name="acc2")
+                    nc.tensor.matmul_mx(
+                        out=acc[:],
+                        lhsT=codes[:, rows].bitcast(FP8X4),
+                        lhsT_scale=scales[:, rows],
+                        rhs=w3[:, c * 2 * BANK : (c + 1) * 2 * BANK].bitcast(FP4X4),
+                        rhs_scale=planes3[:, c * BANK : (c + 1) * BANK],
+                        start=True,
+                        stop=True,
+                    )
+                    live["acc2", m, j, c] = acc
+
+        def add_bias3(m):
+            logit = logit_pool.tile([P, PAIR, PIXELS], F32, name="logit")
+            for j in range(PAIR):
+                for c in range(HALVES):
+                    nc.vector.tensor_tensor(
+                        out=logit[:, j, c * BANK : (c + 1) * BANK],
+                        in0=live.pop(("acc2", m, j, c))[:],
+                        in1=b3_rows[:, c * BANK : (c + 1) * BANK],
+                        op=ALU.add,
+                    )
+            live["logit", m] = logit
+
+        def abs_and_sum(m, j):
+            if ("abs_l", m) not in live:
+                live["abs_l", m] = abs_pool.tile([P, PAIR, PIXELS], F32, name="abs_l")
+            i = m * PAIR + j
+            logit = live["logit", m][:, j, :]
+            abs_l = live["abs_l", m][:, j, :]
+            if m in (ABS0_ON_VECTOR, ABS1_ON_VECTOR)[j]:
+                nc.vector.scalar_tensor_tensor(
+                    out=abs_l,
+                    in0=logit,
+                    scalar=-1.0,
+                    in1=logit,
+                    op0=ALU.mult,
+                    op1=ALU.max,
+                    accum_out=sum_abs[:, i : i + 1],
                 )
-                live["acc2", i, c] = acc
-
-        def add_bias3(i):
-            logit = logit_pool.tile([P, PIXELS], F32, name="logit")
-            for c in range(HALVES):
-                nc.vector.tensor_tensor(
-                    out=logit[:, c * BANK : (c + 1) * BANK],
-                    in0=live.pop(("acc2", i, c))[:],
-                    in1=b3_rows[:, c * BANK : (c + 1) * BANK],
-                    op=ALU.add,
+            else:
+                nc.scalar.activation(
+                    out=abs_l, in_=logit, func=ACT.Abs, accum_out=sum_abs[:, i : i + 1]
                 )
-            live["logit", i] = logit
 
-        def abs_on_vector_part(i):
-            logit = live["logit", i]
-            abs_l = live["abs_l", i]
-            nc.vector.scalar_tensor_tensor(
-                out=abs_l[:, ABS_ON_SCALAR:],
-                in0=logit[:, ABS_ON_SCALAR:],
-                scalar=-1.0,
-                in1=logit[:, ABS_ON_SCALAR:],
-                op0=ALU.mult,
-                op1=ALU.max,
-                accum_out=sum_abs_vector[:, i : i + 1],
-            )
-
-        def abs_on_scalar(i):
-            live["abs_l", i] = abs_pool.tile([P, PIXELS], F32, name="abs_l")
-            nc.scalar.activation(
-                out=live["abs_l", i][:, :ABS_ON_SCALAR],
-                in_=live["logit", i][:, :ABS_ON_SCALAR],
-                func=ACT.Abs,
-                accum_out=sum_abs_scalar[:, i : i + 1],
-            )
-
-        def exp_minus_abs(i):
-            abs_l = live["abs_l", i]
+        def exp_minus_abs(m):
+            abs_l = live["abs_l", m]
             nc.scalar.activation(out=abs_l[:], in_=abs_l[:], func=ACT.Exp, scale=-1.0)
 
         def dot_with_x(i):
-            logit = live.pop(("logit", i))
+            m, j = divmod(i, PAIR)
+            logit = live["logit", m][:, j, :]
             nc.vector.scalar_tensor_tensor(
-                out=logit[:],
-                in0=x_loads[i // X_LOAD_TILES][:, i % X_LOAD_TILES, :],
+                out=logit,
+                in0=live["x", m][:, j, :],
                 scalar=-0.5,
-                in1=logit[:],
+                in1=logit,
                 op0=ALU.add,
                 op1=ALU.mult,
                 accum_out=sum_xl[:, i : i + 1],
             )
+            if j == PAIR - 1 and m + X_AHEAD < N_PAIRS:
+                load_x(m + X_AHEAD)
 
-        def log1p(i):
-            e = live.pop(("abs_l", i))
-            nc.scalar.activation(
-                out=e[:], in_=e[:], func=ACT.Ln, bias=1.0, accum_out=sum_log[:, i : i + 1]
-            )
+        def logarithms(group):
+            for m in group:
+                e = live.pop(("abs_l", m))
+                for j in range(PAIR):
+                    i = m * PAIR + j
+                    nc.scalar.activation(
+                        out=e[:, j, :],
+                        in_=e[:, j, :],
+                        func=ACT.Ln,
+                        bias=1.0,
+                        accum_out=sum_log[:, i : i + 1],
+                    )
 
-        def run(step, i):
-            if 0 <= i < N_TILES:
-                step(i)
+        ALL = [(q, t) for q in range(1, len(QUADS)) for t in range(PACK)]
+        CUM = [sum(STEPS[:m]) for m in range(N_PAIRS + 1)]
 
-        for n in range(N_TILES + LAG_EXP_ABS):
-            run(logit_matmuls, n - LAG_LOGITS)
-            run(hidden_matmul, n - LAG_HIDDEN)
-            run(copy_d, n - LAG_COPY_D)
-            run(elu_and_transpose, n - LAG_ELU)
-            run(copy_h, n - LAG_COPY_H)
-            run(add_bias2, n - LAG_BIAS2)
-            run(exp_v, n - LAG_EXP)
-            run(add_bias3, n - LAG_BIAS3)
-            run(abs_on_scalar, n - LAG_ABS)
-            run(abs_on_vector_part, n - LAG_ABS)
-            run(exp_minus_abs, n - LAG_EXP_ABS)
-            run(transpose_h, n)
-            done = n - LAG_EXP_ABS + 1
-            if done > 0 and done % GROUP == 0:
-                for i in range(done - GROUP, done):
+        def hidden_steps(m):
+            return ALL[CUM[m]:CUM[m + 1]]
+
+        nxt = [0]
+
+        def issue(upto):
+            while nxt[0] < min(upto, len(ALL)):
+                hidden_matmul(*ALL[nxt[0]])
+                nxt[0] += 1
+
+        transpose_h(0)
+        transpose_h(1)
+        copy_h(0)
+        quantize_h(0)
+        for t in range(PACK):
+            hidden_matmul(0, t)
+        copy_h(1)
+        quantize_h(1)
+        issue(2)
+        for m in PREP[0]:
+            transpose_h(m)
+        for t in range(PACK):
+            exp_and_relu(0, t)
+
+        dots = 0
+        for m in range(N_PAIRS):
+            elu(m)
+            for other in PREP[m]:
+                copy_h(other)
+            logit_matmuls(m)
+            if m > 0 and m - 1 in ABS1_ON_VECTOR:
+                abs_and_sum(m - 1, 1)
+            for other in PREP[m]:
+                quantize_h(other)
+            if m == 0:
+                add_bias3(m)
+            for n in range(CUM[m], CUM[m + 1]):
+                exp_and_relu(*ALL[n])
+                if n + 2 < CUM[m + 1]:
+                    issue(n + 3)
+            for other in (PREP + [[]])[m + 1]:
+                transpose_h(other)
+            issue(CUM[m + 1] + 2)
+            if m > 0 and m - 1 not in ABS1_ON_VECTOR:
+                abs_and_sum(m - 1, 1)
+            if m > 0:
+                exp_minus_abs(m - 1)
+            if m == GROUP:
+                logarithms(range(GROUP))
+            if m > 0:
+                add_bias3(m)
+            abs_and_sum(m, 0)
+            if m + 1 < N_PAIRS:
+                for i in range(dots, dots + DOTS[m]):
                     dot_with_x(i)
-                    log1p(i)
+                dots += DOTS[m]
+        abs_and_sum(N_PAIRS - 1, 1)
+        exp_minus_abs(N_PAIRS - 1)
+        logarithms(range(GROUP, N_PAIRS))
+        for i in range(dots, N_TILES):
+            dot_with_x(i)
 
-        sum_abs = keep.tile([P, N_TILES], F32)
-        nc.vector.tensor_tensor(
-            out=sum_abs[:], in0=sum_abs_vector[:], in1=sum_abs_scalar[:], op=ALU.add
-        )
         linear = keep.tile([P, N_TILES], F32)
         nc.vector.scalar_tensor_tensor(
             out=linear[:], in0=sum_abs[:], scalar=-0.5, in1=sum_xl[:], op0=ALU.mult, op1=ALU.add

@@ -23,16 +23,15 @@ PAIR = 2
 N_PAIRS = N_TILES // PAIR
 QUADS = [(0,), (1,)] + [(m, m + 1) for m in range(2, N_PAIRS, 2)]
 GROUP = 6
-COPY_ON_SCALAR = (0, 1, 2, 3, 4, 5)
+COPY_ON_SCALAR = (0, 1)
 RELU_ON_VECTOR = (0,)
-ABS0_ON_VECTOR = (5, 6, 7, 8)
-ABS1_ON_VECTOR = tuple(range(N_PAIRS))
-PREP = [[2, 3], [4, 5], [6, 7], [8], [9], [10], [11], [], [], [], [], []]
-STEPS = [4, 4, 4, 2, 2, 2, 2, 0, 2, 2, 0, 0]
-DOTS = [0, 0, 0, 0, 0, 0, 0, 2, 2, 2, 2]
+ABS1_ON_SCALAR = (0, 1)
+ABS0_ON_VECTOR = (6, 7, 8, 9, 10)
 LOGIT_BUFS = 9
-ABS_BUFS = 7
-ER_BUFS = 2
+ABS_BUFS = 8
+PREP_AHEAD = 5
+HIDDEN_LATE = 3
+DOTS_FIRST = 6
 H_AHEAD = 6
 X_AHEAD = 7
 
@@ -54,10 +53,8 @@ def tile_gmvae_pb_kernel(
         ring2 = stack.enter_context(tc.tile_pool(name="ring2", bufs=2))
         logit_pool = stack.enter_context(tc.tile_pool(name="logit", bufs=LOGIT_BUFS))
         abs_pool = stack.enter_context(tc.tile_pool(name="abs", bufs=ABS_BUFS))
-        er_pool = stack.enter_context(tc.tile_pool(name="er", bufs=ER_BUFS))
         banks_t = stack.enter_context(tc.psum_pool(name="banks_t", bufs=2))
-        banks_1 = stack.enter_context(tc.psum_pool(name="banks_1", bufs=2))
-        banks_2 = stack.enter_context(tc.psum_pool(name="banks_2", bufs=2 * HALVES))
+        banks = stack.enter_context(tc.psum_pool(name="banks", bufs=6))
 
         planes2_raw = keep.tile([P, HIDDEN], U8, align_bytes=64)
         planes3 = keep.tile([P, PIXELS], U8, align_bytes=64)
@@ -164,7 +161,7 @@ def tile_gmvae_pb_kernel(
 
         def hidden_matmul(q, t):
             width = len(QUADS[q]) * PAIR * P
-            acc = banks_1.tile([P, BANK], F32, name="acc1") if q else banks_2.tile([P, BANK], F32, name="acc2")
+            acc = banks.tile([P, BANK], F32, name="acc")
             nc.tensor.matmul_mx(
                 out=acc[:, :width],
                 lhsT=w2[:, t, :].bitcast(FP4X4),
@@ -179,8 +176,8 @@ def tile_gmvae_pb_kernel(
         def exp_and_relu(q, t):
             width = len(QUADS[q]) * PAIR * P
             if t == 0:
-                live["exp_v", q] = er_pool.tile([P, PACK, BANK], F32, name="exp_v")
-                live["relu_v", q] = er_pool.tile([P, PACK, BANK], F32, name="relu_v")
+                live["exp_v", q] = logit_pool.tile([P, PACK, BANK], F32, name="logit")
+                live["relu_v", q] = abs_pool.tile([P, PACK, BANK], F32, name="abs_l")
             acc = live.pop(("acc1", q, t))
             nc.scalar.activation(
                 out=live["exp_v", q][:, t, :width],
@@ -218,18 +215,22 @@ def tile_gmvae_pb_kernel(
             )
             live["d_grouped", m] = d_grouped
 
-        def logit_matmuls(m):
-            codes = ring2.tile([P, PAIR * P], U32, align_bytes=64, name="d_codes")
-            scales = ring2.tile([P, PAIR * P], U8, align_bytes=64, name="d_scales")
+        def quantize_d(m):
+            codes = keep.tile([P, PAIR * P], U32, align_bytes=64, name="d_codes%d" % m)
+            scales = keep.tile([P, PAIR * P], U8, align_bytes=64, name="d_scales%d" % m)
             nc.vector.quantize_mx(
                 out=codes[:].bitcast(FP8X4),
                 scales=scales[:],
                 in_=live.pop(("d_grouped", m))[:].rearrange("p r t -> p (r t)"),
             )
-            for j in range(PAIR):
+            live["d", m] = codes, scales
+
+        def logit_matmuls(m):
+            codes, scales = live.pop(("d", m))
+            for j in reversed(range(PAIR)):
                 rows = slice(j * P, (j + 1) * P)
                 for c in range(HALVES):
-                    acc = banks_2.tile([P, BANK], F32, name="acc2")
+                    acc = banks.tile([P, BANK], F32, name="acc")
                     nc.tensor.matmul_mx(
                         out=acc[:],
                         lhsT=codes[:, rows].bitcast(FP8X4),
@@ -243,7 +244,7 @@ def tile_gmvae_pb_kernel(
 
         def add_bias3(m):
             logit = logit_pool.tile([P, PAIR, PIXELS], F32, name="logit")
-            for j in range(PAIR):
+            for j in reversed(range(PAIR)):
                 for c in range(HALVES):
                     nc.vector.tensor_tensor(
                         out=logit[:, j, c * BANK : (c + 1) * BANK],
@@ -259,7 +260,7 @@ def tile_gmvae_pb_kernel(
             i = m * PAIR + j
             logit = live["logit", m][:, j, :]
             abs_l = live["abs_l", m][:, j, :]
-            if m in (ABS0_ON_VECTOR, ABS1_ON_VECTOR)[j]:
+            if m in ABS0_ON_VECTOR or j == 1 and m not in ABS1_ON_SCALAR:
                 nc.vector.scalar_tensor_tensor(
                     out=abs_l,
                     in0=logit,
@@ -306,69 +307,67 @@ def tile_gmvae_pb_kernel(
                         accum_out=sum_log[:, i : i + 1],
                     )
 
-        ALL = [(q, t) for q in range(1, len(QUADS)) for t in range(PACK)]
-        CUM = [sum(STEPS[:m]) for m in range(N_PAIRS + 1)]
+        def prepare(m):
+            transpose_h(m)
+            copy_h(m)
+            quantize_h(m)
 
-        def hidden_steps(m):
-            return ALL[CUM[m]:CUM[m + 1]]
+        def hidden(q):
+            for t in range(PACK):
+                hidden_matmul(q, t)
+                exp_and_relu(q, t)
 
-        nxt = [0]
+        ready = [0]
 
-        def issue(upto):
-            while nxt[0] < min(upto, len(ALL)):
-                hidden_matmul(*ALL[nxt[0]])
-                nxt[0] += 1
+        def hidden_of(m):
+            if place(m)[0] >= ready[0] and m == QUADS[place(m)[0]][-1]:
+                hidden(place(m)[0])
+                ready[0] += 1
+
+        def logits(m):
+            logit_matmuls(m)
+            add_bias3(m)
+            abs_and_sum(m, 1)
+            abs_and_sum(m, 0)
+            exp_minus_abs(m)
+
+        def copy_next(m):
+            copy_h(m)
+            if m + 2 < N_PAIRS:
+                transpose_h(m + 2)
 
         transpose_h(0)
         transpose_h(1)
-        copy_h(0)
-        quantize_h(0)
-        for t in range(PACK):
-            hidden_matmul(0, t)
-        copy_h(1)
-        quantize_h(1)
-        issue(2)
-        for m in PREP[0]:
-            transpose_h(m)
-        for t in range(PACK):
-            exp_and_relu(0, t)
-
+        for m in range(PREP_AHEAD):
+            copy_next(m)
+            quantize_h(m)
+            hidden_of(m)
+        for m in range(N_PAIRS - HIDDEN_LATE):
+            elu(m)
+            o = m + PREP_AHEAD
+            if o < N_PAIRS:
+                copy_next(o)
+            quantize_d(m)
+            if o < N_PAIRS:
+                quantize_h(o)
+                hidden_of(o)
         dots = 0
         for m in range(N_PAIRS):
-            elu(m)
-            for other in PREP[m]:
-                copy_h(other)
             logit_matmuls(m)
-            if m > 0 and m - 1 in ABS1_ON_VECTOR:
-                abs_and_sum(m - 1, 1)
-            for other in PREP[m]:
-                quantize_h(other)
-            if m == 0:
-                add_bias3(m)
-            for n in range(CUM[m], CUM[m + 1]):
-                exp_and_relu(*ALL[n])
-                if n + 2 < CUM[m + 1]:
-                    issue(n + 3)
-            for other in (PREP + [[]])[m + 1]:
-                transpose_h(other)
-            issue(CUM[m + 1] + 2)
-            if m > 0 and m - 1 not in ABS1_ON_VECTOR:
-                abs_and_sum(m - 1, 1)
-            if m > 0:
-                exp_minus_abs(m - 1)
-            if m == GROUP:
-                logarithms(range(GROUP))
-            if m > 0:
-                add_bias3(m)
+            add_bias3(m)
+            abs_and_sum(m, 1)
             abs_and_sum(m, 0)
-            if m + 1 < N_PAIRS:
-                for i in range(dots, dots + DOTS[m]):
+            exp_minus_abs(m)
+            o = m + N_PAIRS - HIDDEN_LATE
+            if o < N_PAIRS:
+                elu(o)
+                quantize_d(o)
+            if m == GROUP - 1:
+                logarithms(range(GROUP))
+                for i in range(DOTS_FIRST):
                     dot_with_x(i)
-                dots += DOTS[m]
-        abs_and_sum(N_PAIRS - 1, 1)
-        exp_minus_abs(N_PAIRS - 1)
         logarithms(range(GROUP, N_PAIRS))
-        for i in range(dots, N_TILES):
+        for i in range(DOTS_FIRST, N_TILES):
             dot_with_x(i)
 
         linear = keep.tile([P, N_TILES], F32)

@@ -32,7 +32,6 @@ ABS_BUFS = 8
 PREP_AHEAD = 5
 HIDDEN_LATE = 3
 DOTS_FIRST = 6
-H_AHEAD = 6
 X_AHEAD = 7
 
 FLOPS = 2 * BATCH * HIDDEN * (HIDDEN + PIXELS)
@@ -48,7 +47,7 @@ def tile_gmvae_pb_kernel(
     with ExitStack() as stack:
         stack.enter_context(tc.manual_schedule())
         keep = stack.enter_context(tc.tile_pool(name="keep", bufs=1))
-        h_pool = stack.enter_context(tc.tile_pool(name="h", bufs=H_AHEAD))
+        h_pool = stack.enter_context(tc.tile_pool(name="h", bufs=N_PAIRS))
         x_pool = stack.enter_context(tc.tile_pool(name="x", bufs=X_AHEAD))
         ring2 = stack.enter_context(tc.tile_pool(name="ring2", bufs=2))
         logit_pool = stack.enter_context(tc.tile_pool(name="logit", bufs=LOGIT_BUFS))
@@ -99,7 +98,7 @@ def tile_gmvae_pb_kernel(
         )
         load_scales(dw3_scales, planes3)
         nc.sync.dma_start(out=b3_rows[:], in_=db3.partition_broadcast(P))
-        for m in range(4, H_AHEAD):
+        for m in range(4, N_PAIRS):
             load_h(m)
         for m in range(X_AHEAD):
             load_x(m)
@@ -129,8 +128,6 @@ def tile_gmvae_pb_kernel(
                         h_t[:, j, u, :], words[:, j, u : HIDDEN // 2 : 2], ident[:]
                     )
             live["h_t", m] = h_t
-            if m + H_AHEAD < N_PAIRS:
-                load_h(m + H_AHEAD)
 
         def copy_h(m):
             h_grouped = ring2.tile([P, PAIR * P * PACK], BF16, align_bytes=64, name="h_grouped")

@@ -22,17 +22,16 @@ HALVES = PIXELS // BANK
 PAIR = 2
 N_PAIRS = N_TILES // PAIR
 QUADS = [(0,), (1,)] + [(m, m + 1) for m in range(2, N_PAIRS, 2)]
-GROUP = 6
-COPY_ON_SCALAR = (0, 1)
-RELU_ON_VECTOR = (0,)
-ABS1_ON_SCALAR = (0, 1)
-ABS0_ON_VECTOR = (6, 7, 8, 9, 10)
-LOGIT_BUFS = 9
-ABS_BUFS = 8
+COPY_ON_SCALAR = (0,)
+RELU_ON_VECTOR = ()
+ABS_ON_VECTOR = (7, 15, 19, 20, 21, 22, 23)
 PREP_AHEAD = 5
 HIDDEN_LATE = 3
-DOTS_FIRST = 6
-X_AHEAD = 7
+X_AHEAD = 3
+H_CHUNK = 4
+DOTS = (0,) * 6 + (1,) * 6
+PROD = tuple(range(8))
+LAG_PROD = 1
 
 FLOPS = 2 * BATCH * HIDDEN * (HIDDEN + PIXELS)
 
@@ -47,11 +46,8 @@ def tile_gmvae_pb_kernel(
     with ExitStack() as stack:
         stack.enter_context(tc.manual_schedule())
         keep = stack.enter_context(tc.tile_pool(name="keep", bufs=1))
-        h_pool = stack.enter_context(tc.tile_pool(name="h", bufs=N_PAIRS))
         x_pool = stack.enter_context(tc.tile_pool(name="x", bufs=X_AHEAD))
-        ring2 = stack.enter_context(tc.tile_pool(name="ring2", bufs=2))
-        logit_pool = stack.enter_context(tc.tile_pool(name="logit", bufs=LOGIT_BUFS))
-        abs_pool = stack.enter_context(tc.tile_pool(name="abs", bufs=ABS_BUFS))
+        big_pool = stack.enter_context(tc.tile_pool(name="big", bufs=2 * N_PAIRS))
         banks_t = stack.enter_context(tc.psum_pool(name="banks_t", bufs=2))
         banks = stack.enter_context(tc.psum_pool(name="banks", bufs=6))
 
@@ -63,6 +59,14 @@ def tile_gmvae_pb_kernel(
         make_identity(nc, ident[:])
 
         live = {}
+
+        def big_tile(shape, dtype):
+            big = big_pool.tile(shape, dtype, align_bytes=64, name="big")
+            return big
+
+        h_loads = [big_tile([P, H_CHUNK * PAIR, HIDDEN], BF16) for n in range(N_PAIRS // H_CHUNK)]
+        grouped = big_tile([P, 4, PAIR * P * PACK], BF16)
+        h_quant = big_tile([P, 4 * BANK], U32)
 
         w2_raw = keep.tile([P, 2 * HIDDEN], U8, align_bytes=64)
         w2 = keep.tile([P, PACK, 2 * P], U8, align_bytes=64)
@@ -77,9 +81,12 @@ def tile_gmvae_pb_kernel(
             for r in range(4):
                 nc.sync.dma_start(out=planes[:].bitcast(I32)[r:P:32, :], in_=rows[r:16:4, :])
 
+        def h_pair(m):
+            first = m % H_CHUNK * PAIR
+            return h_loads[m // H_CHUNK][:, first : first + PAIR, :]
+
         def load_h(m):
-            live["h", m] = h_pool.tile([P, PAIR, HIDDEN], BF16, name="h_load")
-            nc.sync.dma_start(out=live["h", m][:], in_=h_rows[:, m * PAIR : (m + 1) * PAIR, :])
+            nc.sync.dma_start(out=h_pair(m), in_=h_rows[:, m * PAIR : (m + 1) * PAIR, :])
 
         def load_x(m):
             live["x", m] = x_pool.tile([P, PAIR, PIXELS], BF16, name="x_load")
@@ -120,7 +127,7 @@ def tile_gmvae_pb_kernel(
         sum_abs = keep.tile([P, N_TILES], F32)
         sum_log = keep.tile([P, N_TILES], F32)
         def transpose_h(m):
-            words = live.pop(("h", m))[:].bitcast(F32)
+            words = h_pair(m).bitcast(F32)
             h_t = banks_t.tile([P, PAIR, 2, P], F32, name="h_t")
             for j in range(PAIR):
                 for u in range(2):
@@ -130,8 +137,8 @@ def tile_gmvae_pb_kernel(
             live["h_t", m] = h_t
 
         def copy_h(m):
-            h_grouped = ring2.tile([P, PAIR * P * PACK], BF16, align_bytes=64, name="h_grouped")
-            out = h_grouped[:].bitcast(F32).rearrange("p (j r u) -> p j r u", j=PAIR, u=2)
+            h_grouped = grouped[:, m % 2, :]
+            out = h_grouped.bitcast(F32).rearrange("p (j r u) -> p j r u", j=PAIR, u=2)
             in_ = live.pop(("h_t", m))[:].rearrange("p j u r -> p j r u")
             if m in COPY_ON_SCALAR:
                 nc.scalar.copy(out=out, in_=in_)
@@ -148,12 +155,14 @@ def tile_gmvae_pb_kernel(
         def quantize_h(m):
             q, cols = place(m)
             if m == QUADS[q][0]:
-                live["h_codes", q] = ring2.tile([P, BANK], U32, align_bytes=64, name="h_codes")
-                live["h_scales", q] = ring2.tile([P, BANK], U8, align_bytes=64, name="h_scales")
+                first = q % 2 * BANK
+                live["h_codes", q] = h_quant[:, first : first + BANK]
+                first = 2 * BANK + q % 2 * BANK // 4
+                live["h_scales", q] = h_quant[:, first : first + BANK // 4].bitcast(U8)
             nc.vector.quantize_mx(
                 out=live["h_codes", q][:, cols].bitcast(FP8X4),
                 scales=live["h_scales", q][:, cols],
-                in_=live.pop(("h_grouped", m))[:],
+                in_=live.pop(("h_grouped", m)),
             )
 
         def hidden_matmul(q, t):
@@ -173,8 +182,8 @@ def tile_gmvae_pb_kernel(
         def exp_and_relu(q, t):
             width = len(QUADS[q]) * PAIR * P
             if t == 0:
-                live["exp_v", q] = logit_pool.tile([P, PACK, BANK], F32, name="logit")
-                live["relu_v", q] = abs_pool.tile([P, PACK, BANK], F32, name="abs_l")
+                live["exp_v", q] = big_tile([P, PACK, BANK], F32)
+                live["relu_v", q] = big_tile([P, PACK, BANK], F32)
             acc = live.pop(("acc1", q, t))
             nc.scalar.activation(
                 out=live["exp_v", q][:, t, :width],
@@ -201,9 +210,9 @@ def tile_gmvae_pb_kernel(
 
         def elu(m):
             q, cols = place(m)
-            d_grouped = ring2.tile([P, PAIR * P, PACK], BF16, align_bytes=64, name="d_grouped")
+            d_grouped = grouped[:, 2 + m % 2, :]
             nc.vector.scalar_tensor_tensor(
-                out=d_grouped[:],
+                out=d_grouped.rearrange("p (r t) -> p r t", t=PACK),
                 in0=live["exp_v", q][:, :, cols].rearrange("p t r -> p r t"),
                 scalar=-1.0,
                 in1=live["relu_v", q][:, :, cols].rearrange("p t r -> p r t"),
@@ -218,7 +227,7 @@ def tile_gmvae_pb_kernel(
             nc.vector.quantize_mx(
                 out=codes[:].bitcast(FP8X4),
                 scales=scales[:],
-                in_=live.pop(("d_grouped", m))[:].rearrange("p r t -> p (r t)"),
+                in_=live.pop(("d_grouped", m)),
             )
             live["d", m] = codes, scales
 
@@ -240,7 +249,7 @@ def tile_gmvae_pb_kernel(
                     live["acc2", m, j, c] = acc
 
         def add_bias3(m):
-            logit = logit_pool.tile([P, PAIR, PIXELS], F32, name="logit")
+            logit = big_tile([P, PAIR, PIXELS], F32)
             for j in reversed(range(PAIR)):
                 for c in range(HALVES):
                     nc.vector.tensor_tensor(
@@ -253,11 +262,11 @@ def tile_gmvae_pb_kernel(
 
         def abs_and_sum(m, j):
             if ("abs_l", m) not in live:
-                live["abs_l", m] = abs_pool.tile([P, PAIR, PIXELS], F32, name="abs_l")
+                live["abs_l", m] = big_tile([P, PAIR, PIXELS], F32)
             i = m * PAIR + j
             logit = live["logit", m][:, j, :]
             abs_l = live["abs_l", m][:, j, :]
-            if m in ABS0_ON_VECTOR or j == 1 and m not in ABS1_ON_SCALAR:
+            if i in ABS_ON_VECTOR:
                 nc.vector.scalar_tensor_tensor(
                     out=abs_l,
                     in0=logit,
@@ -274,7 +283,14 @@ def tile_gmvae_pb_kernel(
 
         def exp_minus_abs(m):
             abs_l = live["abs_l", m]
-            nc.scalar.activation(out=abs_l[:], in_=abs_l[:], func=ACT.Exp, scale=-1.0)
+            nc.scalar.activation(out=abs_l[:], in_=abs_l[:], func=ACT.Sigmoid)
+
+        def products(m):
+            sig = live["abs_l", m]
+            for j in range(PAIR):
+                nc.gpsimd.tensor_tensor(
+                    out=sig[:, j, :BANK], in0=sig[:, j, :BANK], in1=sig[:, j, BANK:], op=ALU.mult
+                )
 
         def dot_with_x(i):
             m, j = divmod(i, PAIR)
@@ -294,20 +310,15 @@ def tile_gmvae_pb_kernel(
         def logarithms(group):
             for m in group:
                 e = live.pop(("abs_l", m))
+                width = BANK if m in PROD else PIXELS
                 for j in range(PAIR):
                     i = m * PAIR + j
                     nc.scalar.activation(
-                        out=e[:, j, :],
-                        in_=e[:, j, :],
+                        out=e[:, j, :width],
+                        in_=e[:, j, :width],
                         func=ACT.Ln,
-                        bias=1.0,
                         accum_out=sum_log[:, i : i + 1],
                     )
-
-        def prepare(m):
-            transpose_h(m)
-            copy_h(m)
-            quantize_h(m)
 
         def hidden(q):
             for t in range(PACK):
@@ -320,13 +331,6 @@ def tile_gmvae_pb_kernel(
             if place(m)[0] >= ready[0] and m == QUADS[place(m)[0]][-1]:
                 hidden(place(m)[0])
                 ready[0] += 1
-
-        def logits(m):
-            logit_matmuls(m)
-            add_bias3(m)
-            abs_and_sum(m, 1)
-            abs_and_sum(m, 0)
-            exp_minus_abs(m)
 
         def copy_next(m):
             copy_h(m)
@@ -354,17 +358,22 @@ def tile_gmvae_pb_kernel(
             add_bias3(m)
             abs_and_sum(m, 1)
             abs_and_sum(m, 0)
-            exp_minus_abs(m)
+            if m > 0:
+                exp_minus_abs(m - 1)
+                if m - 1 in PROD:
+                    products(m - 1)
             o = m + N_PAIRS - HIDDEN_LATE
             if o < N_PAIRS:
                 elu(o)
                 quantize_d(o)
-            if m == GROUP - 1:
-                logarithms(range(GROUP))
-                for i in range(DOTS_FIRST):
-                    dot_with_x(i)
-        logarithms(range(GROUP, N_PAIRS))
-        for i in range(DOTS_FIRST, N_TILES):
+            for i in range(dots, dots + DOTS[m]):
+                dot_with_x(i)
+            dots += DOTS[m]
+        exp_minus_abs(N_PAIRS - 1)
+        if N_PAIRS - 1 in PROD:
+            products(N_PAIRS - 1)
+        logarithms(range(N_PAIRS))
+        for i in range(dots, N_TILES):
             dot_with_x(i)
 
         linear = keep.tile([P, N_TILES], F32)
@@ -372,5 +381,5 @@ def tile_gmvae_pb_kernel(
             out=linear[:], in0=sum_abs[:], scalar=-0.5, in1=sum_xl[:], op0=ALU.mult, op1=ALU.add
         )
         result = keep.tile([P, N_TILES], F32)
-        nc.vector.tensor_tensor(out=result[:], in0=linear[:], in1=sum_log[:], op=ALU.subtract)
+        nc.vector.tensor_tensor(out=result[:], in0=linear[:], in1=sum_log[:], op=ALU.add)
         nc.sync.dma_start(out=out.rearrange("(p i) -> p i", i=N_TILES), in_=result[:])

@@ -24,13 +24,13 @@ N_PAIRS = N_TILES // PAIR
 QUADS = [(0,), (1,)] + [(m, m + 1) for m in range(2, N_PAIRS, 2)]
 COPY_ON_SCALAR = (0,)
 RELU_ON_VECTOR = ()
-ABS_ON_VECTOR = (7, 15, 19, 20, 21, 22, 23)
+ABS_ON_VECTOR = tuple(range(3, N_TILES, 4))
 PREP_AHEAD = 5
-HIDDEN_LATE = 3
+HIDDEN_LATE = 4
 X_AHEAD = 3
 H_CHUNK = 4
 DOTS = (0,) * 6 + (1,) * 6
-PROD = tuple(range(8))
+PROD = tuple(range(9))
 LAG_PROD = 1
 
 FLOPS = 2 * BATCH * HIDDEN * (HIDDEN + PIXELS)
@@ -339,8 +339,13 @@ def tile_gmvae_pb_kernel(
 
         transpose_h(0)
         transpose_h(1)
-        for m in range(PREP_AHEAD):
-            copy_next(m)
+        copy_next(0)
+        quantize_h(0)
+        hidden_of(0)
+        copy_next(1)
+        for m in range(1, PREP_AHEAD):
+            if m + 1 < PREP_AHEAD:
+                copy_next(m + 1)
             quantize_h(m)
             hidden_of(m)
         for m in range(N_PAIRS - HIDDEN_LATE):
@@ -354,18 +359,19 @@ def tile_gmvae_pb_kernel(
                 hidden_of(o)
         dots = 0
         for m in range(N_PAIRS):
+            o = m + N_PAIRS - HIDDEN_LATE
+            if o < N_PAIRS:
+                elu(o)
             logit_matmuls(m)
             add_bias3(m)
+            if o < N_PAIRS:
+                quantize_d(o)
             abs_and_sum(m, 1)
             abs_and_sum(m, 0)
             if m > 0:
                 exp_minus_abs(m - 1)
                 if m - 1 in PROD:
                     products(m - 1)
-            o = m + N_PAIRS - HIDDEN_LATE
-            if o < N_PAIRS:
-                elu(o)
-                quantize_d(o)
             for i in range(dots, dots + DOTS[m]):
                 dot_with_x(i)
             dots += DOTS[m]

@@ -27,7 +27,7 @@ RELU_ON_VECTOR = ()
 ABS_ON_VECTOR = tuple(range(3, N_TILES, 4))
 PREP_AHEAD = 5
 HIDDEN_LATE = 4
-X_AHEAD = 3
+X_AHEAD = 4
 H_CHUNK = 4
 DOTS = (0,) * 6 + (1,) * 6
 PROD = tuple(range(9))
@@ -98,15 +98,13 @@ def tile_gmvae_pb_kernel(
             out=w2_raw[:].bitcast(I32), in_=dw2_words.rearrange("g p n -> (g p) n").bitcast(I32)
         )
         load_scales(dw2_scales, planes2_raw)
-        for m in range(1, 4):
+        for m in range(1, N_PAIRS):
             load_h(m)
         nc.sync.dma_start(
             out=w3[:].bitcast(I32), in_=dw3_words.rearrange("g p n -> (g p) n").bitcast(I32)
         )
         load_scales(dw3_scales, planes3)
         nc.sync.dma_start(out=b3_rows[:], in_=db3.partition_broadcast(P))
-        for m in range(4, N_PAIRS):
-            load_h(m)
         for m in range(X_AHEAD):
             load_x(m)
 

@@ -24,7 +24,8 @@ N_PAIRS = N_TILES // PAIR
 QUADS = [(0,), (1,)] + [(m, m + 1) for m in range(2, N_PAIRS, 2)]
 COPY_ON_SCALAR = (0,)
 RELU_ON_VECTOR = ()
-ABS_ON_VECTOR = tuple(range(3, N_TILES, 4))
+V_PAIRS = 4
+CLAMP = 20.0
 PREP_AHEAD = 5
 HIDDEN_LATE = 4
 X_AHEAD = 4
@@ -85,21 +86,29 @@ def tile_gmvae_pb_kernel(
             first = m % H_CHUNK * PAIR
             return h_loads[m // H_CHUNK][:, first : first + PAIR, :]
 
-        def load_h(m):
-            nc.sync.dma_start(out=h_pair(m), in_=h_rows[:, m * PAIR : (m + 1) * PAIR, :])
+        def load_h(first, last):
+            tile = h_loads[first // H_CHUNK]
+            start = first % H_CHUNK * PAIR
+            rows = (last - first + 1) * PAIR
+            nc.sync.dma_start(
+                out=tile[:, start : start + rows, :],
+                in_=h_rows[:, first * PAIR : (last + 1) * PAIR, :],
+            )
 
         def load_x(m):
             live["x", m] = x_pool.tile([P, PAIR, PIXELS], BF16, name="x_load")
             nc.sync.dma_start(out=live["x", m][:], in_=x_rows[:, m * PAIR : (m + 1) * PAIR, :])
 
-        nc.scalar.dma_start(out=b2_raw[:], in_=db2.rearrange("(p t) -> p t", t=PACK))
-        load_h(0)
+        nc.gpsimd.dma_start(out=b2_raw[:], in_=db2.rearrange("(p t) -> p t", t=PACK))
+        load_h(0, 0)
         nc.sync.dma_start(
             out=w2_raw[:].bitcast(I32), in_=dw2_words.rearrange("g p n -> (g p) n").bitcast(I32)
         )
         load_scales(dw2_scales, planes2_raw)
-        for m in range(1, N_PAIRS):
-            load_h(m)
+        load_h(1, 1)
+        load_h(2, H_CHUNK - 1)
+        for first in range(H_CHUNK, N_PAIRS, H_CHUNK):
+            load_h(first, first + H_CHUNK - 1)
         nc.sync.dma_start(
             out=w3[:].bitcast(I32), in_=dw3_words.rearrange("g p n -> (g p) n").bitcast(I32)
         )
@@ -258,20 +267,23 @@ def tile_gmvae_pb_kernel(
                     )
             live["logit", m] = logit
 
+        def by_clamp(m):
+            return m % V_PAIRS == V_PAIRS - 1
+
         def abs_and_sum(m, j):
             if ("abs_l", m) not in live:
                 live["abs_l", m] = big_tile([P, PAIR, PIXELS], F32)
             i = m * PAIR + j
             logit = live["logit", m][:, j, :]
             abs_l = live["abs_l", m][:, j, :]
-            if i in ABS_ON_VECTOR:
-                nc.vector.scalar_tensor_tensor(
+            if by_clamp(m):
+                nc.vector.tensor_scalar(
                     out=abs_l,
                     in0=logit,
-                    scalar=-1.0,
-                    in1=logit,
-                    op0=ALU.mult,
-                    op1=ALU.max,
+                    scalar1=CLAMP,
+                    scalar2=None,
+                    op0=ALU.min,
+                    op1=ALU.add,
                     accum_out=sum_abs[:, i : i + 1],
                 )
             else:
@@ -281,7 +293,8 @@ def tile_gmvae_pb_kernel(
 
         def exp_minus_abs(m):
             abs_l = live["abs_l", m]
-            nc.scalar.activation(out=abs_l[:], in_=abs_l[:], func=ACT.Sigmoid)
+            sign = -1.0 if by_clamp(m) else 1.0
+            nc.scalar.activation(out=abs_l[:], in_=abs_l[:], func=ACT.Sigmoid, scale=sign)
 
         def products(m):
             sig = live["abs_l", m]
@@ -296,7 +309,7 @@ def tile_gmvae_pb_kernel(
             nc.vector.scalar_tensor_tensor(
                 out=logit,
                 in0=live["x", m][:, j, :],
-                scalar=-0.5,
+                scalar=-1.0 if by_clamp(m) else -0.5,
                 in1=logit,
                 op0=ALU.add,
                 op1=ALU.mult,
@@ -381,9 +394,18 @@ def tile_gmvae_pb_kernel(
             dot_with_x(i)
 
         linear = keep.tile([P, N_TILES], F32)
-        nc.vector.scalar_tensor_tensor(
-            out=linear[:], in0=sum_abs[:], scalar=-0.5, in1=sum_xl[:], op0=ALU.mult, op1=ALU.add
-        )
+        period = V_PAIRS * PAIR
+        for factor, cols in (
+            (-0.5, slice(0, period - PAIR)),
+            (1.0, slice(period - PAIR, period)),
+        ):
+            out_cols, abs_cols, xl_cols = (
+                t[:].rearrange("p (n i) -> p n i", i=period)[:, :, cols]
+                for t in (linear, sum_abs, sum_xl)
+            )
+            nc.vector.scalar_tensor_tensor(
+                out=out_cols, in0=abs_cols, scalar=factor, in1=xl_cols, op0=ALU.mult, op1=ALU.add
+            )
         result = keep.tile([P, N_TILES], F32)
         nc.vector.tensor_tensor(out=result[:], in0=linear[:], in1=sum_log[:], op=ALU.add)
         nc.sync.dma_start(out=out.rearrange("(p i) -> p i", i=N_TILES), in_=result[:])

from contextlib import ExitStack

import concourse.mybir as mybir
from concourse.masks import make_identity

F32 = mybir.dt.float32
BF16 = mybir.dt.bfloat16
I32 = mybir.dt.int32
U32 = mybir.dt.uint32
U8 = mybir.dt.uint8
FP8X4 = mybir.dt.float8_e4m3fn_x4
FP4X4 = mybir.dt.float4_e2m1fn_x4
ALU = mybir.AluOpType
ACT = mybir.ActivationFunctionType

P = 128
PACK = 4
BATCH, HIDDEN, PIXELS = 3072, 512, 1024
N_TILES = BATCH // P
BANK = 512
HALVES = PIXELS // BANK
PAIR = 2
N_PAIRS = N_TILES // PAIR
QUADS = [(0,), (1,)] + [(m, m + 1) for m in range(2, N_PAIRS, 2)]
COPY_ON_SCALAR = (0,)
RELU_ON_VECTOR = ()
V_PAIRS = 4
CLAMP = 20.0
PREP_AHEAD = 5
HIDDEN_LATE = 4
X_AHEAD = 4
H_CHUNK = 4
DOTS = (0,) * 6 + (1,) * 6
PROD = tuple(range(9))
LAG_PROD = 1

FLOPS = 2 * BATCH * HIDDEN * (HIDDEN + PIXELS)


def tile_gmvae_pb_kernel(
    tc, dec_h1, x, dw2_words, dw2_scales, db2, dw3_words, dw3_scales, db3, out
):
    nc = tc.nc
    h_rows = dec_h1.rearrange("(p i) k -> p i k", i=N_TILES)
    x_rows = x.rearrange("(p i) j -> p i j", i=N_TILES)

    with ExitStack() as stack:
        stack.enter_context(tc.manual_schedule())
        keep = stack.enter_context(tc.tile_pool(name="keep", bufs=1))
        x_pool = stack.enter_context(tc.tile_pool(name="x", bufs=X_AHEAD))
        big_pool = stack.enter_context(tc.tile_pool(name="big", bufs=2 * N_PAIRS))
        banks_t = stack.enter_context(tc.psum_pool(name="banks_t", bufs=2))
        banks = stack.enter_context(tc.psum_pool(name="banks", bufs=6))

        planes2_raw = keep.tile([P, HIDDEN], U8, align_bytes=64)
        planes3 = keep.tile([P, PIXELS], U8, align_bytes=64)
        nc.vector.memset(planes2_raw[:].bitcast(I32), 0)
        nc.vector.memset(planes3[:].bitcast(I32), 0)
        ident = keep.tile([P, P], F32)
        make_identity(nc, ident[:])

        live = {}

        def big_tile(shape, dtype):
            big = big_pool.tile(shape, dtype, align_bytes=64, name="big")
            return big

        h_loads = [big_tile([P, H_CHUNK * PAIR, HIDDEN], BF16) for n in range(N_PAIRS // H_CHUNK)]
        grouped = big_tile([P, 4, PAIR * P * PACK], BF16)
        h_quant = big_tile([P, 4 * BANK], U32)

        w2_raw = keep.tile([P, 2 * HIDDEN], U8, align_bytes=64)
        w2 = keep.tile([P, PACK, 2 * P], U8, align_bytes=64)
        planes2 = keep.tile([P, PACK, P], U8, align_bytes=64)
        w3 = keep.tile([P, 2 * PIXELS], U8, align_bytes=64)
        b2_raw = keep.tile([P, PACK], BF16)
        b2 = keep.tile([P, PACK], F32)
        b3_rows = keep.tile([P, PIXELS], BF16)

        def load_scales(scales, planes):
            rows = scales.rearrange("g q n -> (g q) n").bitcast(I32)
            for r in range(4):
                nc.sync.dma_start(out=planes[:].bitcast(I32)[r:P:32, :], in_=rows[r:16:4, :])

        def h_pair(m):
            first = m % H_CHUNK * PAIR
            return h_loads[m // H_CHUNK][:, first : first + PAIR, :]

        def load_h(first, last):
            tile = h_loads[first // H_CHUNK]
            start = first % H_CHUNK * PAIR
            rows = (last - first + 1) * PAIR
            nc.sync.dma_start(
                out=tile[:, start : start + rows, :],
                in_=h_rows[:, first * PAIR : (last + 1) * PAIR, :],
            )

        def load_x(m):
            live["x", m] = x_pool.tile([P, PAIR, PIXELS], BF16, name="x_load")
            nc.sync.dma_start(out=live["x", m][:], in_=x_rows[:, m * PAIR : (m + 1) * PAIR, :])

        nc.gpsimd.dma_start(out=b2_raw[:], in_=db2.rearrange("(p t) -> p t", t=PACK))
        load_h(0, 0)
        nc.sync.dma_start(
            out=w2_raw[:].bitcast(I32), in_=dw2_words.rearrange("g p n -> (g p) n").bitcast(I32)
        )
        load_scales(dw2_scales, planes2_raw)
        load_h(1, 1)
        load_h(2, H_CHUNK - 1)
        for first in range(H_CHUNK, N_PAIRS, H_CHUNK):
            load_h(first, first + H_CHUNK - 1)
        nc.sync.dma_start(
            out=w3[:].bitcast(I32), in_=dw3_words.rearrange("g p n -> (g p) n").bitcast(I32)
        )
        load_scales(dw3_scales, planes3)
        nc.sync.dma_start(out=b3_rows[:], in_=db3.partition_broadcast(P))
        for m in range(X_AHEAD):
            load_x(m)

        warm = keep.tile([P, 2], F32)
        nc.vector.memset(warm[:], 0.0)
        nc.scalar.activation(out=warm[:, 1:2], in_=warm[:, 0:1], func=ACT.Exp)

        nc.vector.tensor_copy(
            out=w2[:].rearrange("p t (m b) -> p t m b", b=2),
            in_=w2_raw[:].rearrange("p (m t b) -> p t m b", t=PACK, b=2),
        )
        nc.vector.tensor_copy(
            out=planes2[:], in_=planes2_raw[:].rearrange("p (m t) -> p t m", t=PACK)
        )
        nc.vector.tensor_copy(out=b2[:], in_=b2_raw[:])

        sum_xl = keep.tile([P, N_TILES], F32)
        sum_abs = keep.tile([P, N_TILES], F32)
        sum_log = keep.tile([P, N_TILES], F32)
        def transpose_h(m):
            words = h_pair(m).bitcast(F32)
            h_t = banks_t.tile([P, PAIR, 2, P], F32, name="h_t")
            for j in range(PAIR):
                for u in range(2):
                    nc.tensor.transpose(
                        h_t[:, j, u, :], words[:, j, u : HIDDEN // 2 : 2], ident[:]
                    )
            live["h_t", m] = h_t

        def copy_h(m):
            h_grouped = grouped[:, m % 2, :]
            out = h_grouped.bitcast(F32).rearrange("p (j r u) -> p j r u", j=PAIR, u=2)
            in_ = live.pop(("h_t", m))[:].rearrange("p j u r -> p j r u")
            if m in COPY_ON_SCALAR:
                nc.scalar.copy(out=out, in_=in_)
            else:
                nc.vector.tensor_copy(out=out, in_=in_)
            live["h_grouped", m] = h_grouped

        def place(m):
            for q, pairs in enumerate(QUADS):
                if m in pairs:
                    first = pairs.index(m) * PAIR * P
                    return q, slice(first, first + PAIR * P)

        def quantize_h(m):
            q, cols = place(m)
            if m == QUADS[q][0]:
                first = q % 2 * BANK
                live["h_codes", q] = h_quant[:, first : first + BANK]
                first = 2 * BANK + q % 2 * BANK // 4
                live["h_scales", q] = h_quant[:, first : first + BANK // 4].bitcast(U8)
            nc.vector.quantize_mx(
                out=live["h_codes", q][:, cols].bitcast(FP8X4),
                scales=live["h_scales", q][:, cols],
                in_=live.pop(("h_grouped", m)),
            )

        def hidden_matmul(q, t):
            width = len(QUADS[q]) * PAIR * P
            acc = banks.tile([P, BANK], F32, name="acc")
            nc.tensor.matmul_mx(
                out=acc[:, :width],
                lhsT=w2[:, t, :].bitcast(FP4X4),
                lhsT_scale=planes2[:, t, :],
                rhs=live["h_codes", q][:, :width].bitcast(FP8X4),
                rhs_scale=live["h_scales", q][:, :width],
                start=True,
                stop=True,
            )
            live["acc1", q, t] = acc

        def exp_and_relu(q, t):
            width = len(QUADS[q]) * PAIR * P
            if t == 0:
                live["exp_v", q] = big_tile([P, PACK, BANK], F32)
                live["relu_v", q] = big_tile([P, PACK, BANK], F32)
            acc = live.pop(("acc1", q, t))
            nc.scalar.activation(
                out=live["exp_v", q][:, t, :width],
                in_=acc[:, :width],
                func=ACT.Exp,
                bias=b2[:, t : t + 1],
            )
            if q in RELU_ON_VECTOR or (q, t) in RELU_ON_VECTOR:
                nc.vector.tensor_scalar(
                    out=live["relu_v", q][:, t, :width],
                    in0=acc[:, :width],
                    scalar1=b2[:, t : t + 1],
                    scalar2=0.0,
                    op0=ALU.add,
                    op1=ALU.max,
                )
            else:
                nc.scalar.activation(
                    out=live["relu_v", q][:, t, :width],
                    in_=acc[:, :width],
                    func=ACT.Relu,
                    bias=b2[:, t : t + 1],
                )

        def elu(m):
            q, cols = place(m)
            d_grouped = grouped[:, 2 + m % 2, :]
            nc.vector.scalar_tensor_tensor(
                out=d_grouped.rearrange("p (r t) -> p r t", t=PACK),
                in0=live["exp_v", q][:, :, cols].rearrange("p t r -> p r t"),
                scalar=-1.0,
                in1=live["relu_v", q][:, :, cols].rearrange("p t r -> p r t"),
                op0=ALU.add,
                op1=ALU.min,
            )
            live["d_grouped", m] = d_grouped

        def quantize_d(m):
            codes = keep.tile([P, PAIR * P], U32, align_bytes=64, name="d_codes%d" % m)
            scales = keep.tile([P, PAIR * P], U8, align_bytes=64, name="d_scales%d" % m)
            nc.vector.quantize_mx(
                out=codes[:].bitcast(FP8X4),
                scales=scales[:],
                in_=live.pop(("d_grouped", m)),
            )
            live["d", m] = codes, scales

        def logit_matmuls(m):
            codes, scales = live.pop(("d", m))
            for j in reversed(range(PAIR)):
                rows = slice(j * P, (j + 1) * P)
                for c in range(HALVES):
                    acc = banks.tile([P, BANK], F32, name="acc")
                    nc.tensor.matmul_mx(
                        out=acc[:],
                        lhsT=codes[:, rows].bitcast(FP8X4),
                        lhsT_scale=scales[:, rows],
                        rhs=w3[:, c * 2 * BANK : (c + 1) * 2 * BANK].bitcast(FP4X4),
                        rhs_scale=planes3[:, c * BANK : (c + 1) * BANK],
                        start=True,
                        stop=True,
                    )
                    live["acc2", m, j, c] = acc

        def add_bias3(m):
            logit = big_tile([P, PAIR, PIXELS], F32)
            for j in reversed(range(PAIR)):
                for c in range(HALVES):
                    nc.vector.tensor_tensor(
                        out=logit[:, j, c * BANK : (c + 1) * BANK],
                        in0=live.pop(("acc2", m, j, c))[:],
                        in1=b3_rows[:, c * BANK : (c + 1) * BANK],
                        op=ALU.add,
                    )
            live["logit", m] = logit

        def by_clamp(m):
            return m % V_PAIRS == V_PAIRS - 1

        def abs_and_sum(m, j):
            if ("abs_l", m) not in live:
                live["abs_l", m] = big_tile([P, PAIR, PIXELS], F32)
            i = m * PAIR + j
            logit = live["logit", m][:, j, :]
            abs_l = live["abs_l", m][:, j, :]
            if by_clamp(m):
                nc.vector.tensor_scalar(
                    out=abs_l,
                    in0=logit,
                    scalar1=CLAMP,
                    scalar2=None,
                    op0=ALU.min,
                    op1=ALU.add,
                    accum_out=sum_abs[:, i : i + 1],
                )
            else:
                nc.scalar.activation(
                    out=abs_l, in_=logit, func=ACT.Abs, accum_out=sum_abs[:, i : i + 1]
                )

        def exp_minus_abs(m):
            abs_l = live["abs_l", m]
            sign = -1.0 if by_clamp(m) else 1.0
            nc.scalar.activation(out=abs_l[:], in_=abs_l[:], func=ACT.Sigmoid, scale=sign)

        def products(m):
            sig = live["abs_l", m]
            for j in range(PAIR):
                nc.gpsimd.tensor_tensor(
                    out=sig[:, j, :BANK], in0=sig[:, j, :BANK], in1=sig[:, j, BANK:], op=ALU.mult
                )

        def dot_with_x(i):
            m, j = divmod(i, PAIR)
            logit = live["logit", m][:, j, :]
            nc.vector.scalar_tensor_tensor(
                out=logit,
                in0=live["x", m][:, j, :],
                scalar=-1.0 if by_clamp(m) else -0.5,
                in1=logit,
                op0=ALU.add,
                op1=ALU.mult,
                accum_out=sum_xl[:, i : i + 1],
            )
            if j == PAIR - 1 and m + X_AHEAD < N_PAIRS:
                load_x(m + X_AHEAD)

        def logarithms(group):
            for m in group:
                e = live.pop(("abs_l", m))
                width = BANK if m in PROD else PIXELS
                for j in range(PAIR):
                    i = m * PAIR + j
                    nc.scalar.activation(
                        out=e[:, j, :width],
                        in_=e[:, j, :width],
                        func=ACT.Ln,
                        accum_out=sum_log[:, i : i + 1],
                    )

        def hidden(q):
            for t in range(PACK):
                hidden_matmul(q, t)
                exp_and_relu(q, t)

        ready = [0]

        def hidden_of(m):
            if place(m)[0] >= ready[0] and m == QUADS[place(m)[0]][-1]:
                hidden(place(m)[0])
                ready[0] += 1

        def copy_next(m):
            copy_h(m)
            if m + 2 < N_PAIRS:
                transpose_h(m + 2)

        transpose_h(0)
        transpose_h(1)
        copy_next(0)
        quantize_h(0)
        hidden_of(0)
        copy_next(1)
        for m in range(1, PREP_AHEAD):
            if m + 1 < PREP_AHEAD:
                copy_next(m + 1)
            quantize_h(m)
            hidden_of(m)
        for m in range(N_PAIRS - HIDDEN_LATE):
            elu(m)
            o = m + PREP_AHEAD
            if o < N_PAIRS:
                copy_next(o)
            quantize_d(m)
            if o < N_PAIRS:
                quantize_h(o)
                hidden_of(o)
        dots = 0
        for m in range(N_PAIRS):
            o = m + N_PAIRS - HIDDEN_LATE
            if o < N_PAIRS:
                elu(o)
            logit_matmuls(m)
            add_bias3(m)
            if o < N_PAIRS:
                quantize_d(o)
            abs_and_sum(m, 1)
            abs_and_sum(m, 0)
            if m > 0:
                exp_minus_abs(m - 1)
                if m - 1 in PROD:
                    products(m - 1)
            for i in range(dots, dots + DOTS[m]):
                dot_with_x(i)
            dots += DOTS[m]
        exp_minus_abs(N_PAIRS - 1)
        if N_PAIRS - 1 in PROD:
            products(N_PAIRS - 1)
        logarithms(range(N_PAIRS))
        for i in range(dots, N_TILES):
            dot_with_x(i)

        linear = keep.tile([P, N_TILES], F32)
        period = V_PAIRS * PAIR
        for factor, cols in (
            (-0.5, slice(0, period - PAIR)),
            (1.0, slice(period - PAIR, period)),
        ):
            out_cols, abs_cols, xl_cols = (
                t[:].rearrange("p (n i) -> p n i", i=period)[:, :, cols]
                for t in (linear, sum_abs, sum_xl)
            )
            nc.vector.scalar_tensor_tensor(
                out=out_cols, in0=abs_cols, scalar=factor, in1=xl_cols, op0=ALU.mult, op1=ALU.add
            )
        result = keep.tile([P, N_TILES], F32)
        nc.vector.tensor_tensor(out=result[:], in0=linear[:], in1=sum_log[:], op=ALU.add)
        nc.sync.dma_start(out=out.rearrange("(p i) -> p i", i=N_TILES), in_=result[:])
